import numpy as np
import ml_dtypes


def mxq(x, axis, fmt="e4m3"):
    dtype, down = {"e4m3": (ml_dtypes.float8_e4m3fn, 7), "e5m2": (ml_dtypes.float8_e5m2, 14)}[fmt]
    v = np.moveaxis(np.asarray(x, np.float32).astype(ml_dtypes.bfloat16).astype(np.float64), axis, -1)
    blocks = v.reshape(v.shape[:-1] + (-1, 32))
    amax = np.abs(blocks).max(-1, keepdims=True)
    byte = np.maximum(np.where(amax > 0, np.frexp(amax)[1] - 1 + 127, 0) - down, 1)
    scale = np.exp2(byte - 127.0)
    codes = (blocks / scale).astype(np.float32).astype(dtype).astype(np.float64)
    return np.moveaxis((codes * scale).reshape(v.shape), -1, axis)


WIDE = False


def mx_kscale(k):
    if not WIDE:
        return np.ones(k)
    levels = np.array([10, -10, 5, -5, 0])
    a = np.random.permutation(np.resize(levels, k // 512 * 4)).reshape(k // 512, 4)
    idx = np.arange(k)
    return np.exp2(a[idx // 512, idx % 128 // 32])


BF16 = ml_dtypes.bfloat16


def bf(x):
    return np.asarray(x, np.float32).astype(BF16)


def f64(x):
    return np.asarray(x).astype(np.float64)


E2M1 = np.array([0.0, 0.5, 1.0, 1.5, 2.0, 3.0, 4.0, 6.0, -0.0, -0.5, -1.0, -1.5, -2.0, -3.0, -4.0, -6.0])


def pack_weight(w, fmt):
    k, n = w.shape
    w = f64(bf(w)).reshape(k // 32, 32, n)
    amax = np.abs(w).max(1)
    if fmt == "e4m3":
        byte = np.frexp(amax)[1] - 1 + 127 - 7
    else:
        mant, ex = np.frexp(amax / 6.0)
        byte = np.where(mant > 0.5, ex, ex - 1) + 127
    byte = np.clip(np.where(amax > 0, byte, 1), 1, 254)
    scaled = (w * np.exp2(127.0 - byte)[:, None, :]).reshape(k, n).astype(np.float32)
    by_word = np.ascontiguousarray(scaled.reshape(k // 512, 128, 4, n).transpose(0, 1, 3, 2))
    if fmt == "e4m3":
        words = by_word.astype(ml_dtypes.float8_e4m3fn).view(np.uint8)
    else:
        c = by_word.astype(ml_dtypes.float4_e2m1fn).view(np.uint8) & 0xF
        words = c[..., 0::2] | (c[..., 1::2] << 4)
    return np.ascontiguousarray(words), np.ascontiguousarray(byte.astype(np.uint8).reshape(k // 512, 16, n))


def unpack_weight(words, scales, fmt):
    g, p, n, _ = words.shape
    if fmt == "e4m3":
        vals = np.ascontiguousarray(words).view(ml_dtypes.float8_e4m3fn).astype(np.float64)
    else:
        nib = np.empty((g, p, n, 4), np.uint8)
        nib[..., 0::2] = words & 0xF
        nib[..., 1::2] = words >> 4
        vals = E2M1[nib]
    vals = vals * np.repeat(np.exp2(scales.astype(np.float64) - 127.0), 8, axis=1)[..., None]
    return vals.transpose(0, 1, 3, 2).reshape(g * 512, n)

def pack4(w):
    words, scales = pack_weight(w, "e2m1")
    return words.reshape(words.shape[0], 128, -1), scales


def unpack4(words, scales):
    return unpack_weight(words.reshape(words.shape[0], 128, -1, 2), scales, "e2m1")


B, I, O, G = 2048, 512, 512, 8
K = I * G


def bspline_basis(d):
    inner = 1.0 - 6.0 * d * d + 6.0 * d * d * d
    outer = 2.0 * (1.0 - d) ** 3
    return np.where(d < 0.5, inner, np.where(d < 1.0, outer, np.zeros_like(d)))


def setup_inputs():
    g = np.linspace(-1.0, 1.0, G)
    s = mx_kscale(I)
    u = s / s.max()
    x_norm = bf(np.tanh(np.random.standard_normal((B, I))) * u)
    spline_weight = bf(np.random.standard_normal((O, I, G)) / np.sqrt(I))
    base_activation = np.random.standard_normal((O, I)) * 4.0 / np.sqrt(I) / u
    words, scales = pack4(base_activation.T)
    grid_points = bf(g + 0.1 * (g[1] - g[0]) * np.random.standard_normal(G))
    return {"x_norm": x_norm,
            "spline_weight": spline_weight,
            "base_activation_words": words,
            "base_activation_scales": scales,
            "grid_points": grid_points}


def reference(x_norm, spline_weight, base_activation_words, base_activation_scales, grid_points):
    t = f64(x_norm)
    d = np.abs(t[:, :, None] - f64(grid_points))
    basis = bspline_basis(d)
    spline_out = mxq(basis.reshape(B, K), 1, "e4m3") @ mxq(f64(spline_weight).reshape(O, K), 1, "e4m3").T
    base_out = mxq(t, 1, "e4m3") @ unpack4(base_activation_words, base_activation_scales)
    return spline_out + 0.1 * base_out

@@ -1,0 +1,231 @@
+from contextlib import ExitStack
+
+import concourse.mybir as mybir
+from concourse.masks import make_identity
+
+F32 = mybir.dt.float32
+BF16 = mybir.dt.bfloat16
+U8 = mybir.dt.uint8
+U32 = mybir.dt.uint32
+I32 = mybir.dt.int32
+FP8X4 = mybir.dt.float8_e4m3fn_x4
+FP4X4 = mybir.dt.float4_e2m1fn_x4
+ACT = mybir.ActivationFunctionType
+ALU = mybir.AluOpType
+
+P = 128
+PACK = 4
+BATCH, FEATURES, OUTPUTS, GRID = 2048, 512, 512, 8
+ROW_TILES = BATCH // P
+TILES_PER_CHUNK = 4
+CHUNKS = ROW_TILES // TILES_PER_CHUNK
+CHUNK_ROWS = TILES_PER_CHUNK * P
+CHUNK_COLS = CHUNK_ROWS * PACK
+STEPS = CHUNKS * GRID
+OUT_BLOCKS = OUTPUTS // P
+
+FLOPS = 2 * BATCH * OUTPUTS * (FEATURES * GRID + FEATURES)
+
+
+def tile_advancedkanlayer_pa_kernel(
+    tc, x_norm, spline_weight, base_activation_words, base_activation_scales, grid_points, out
+):
+    nc = tc.nc
+    x_rows = x_norm.rearrange("(p n) i -> p n i", n=ROW_TILES)
+    out_rows = out.rearrange("(p n) o -> p n o", n=ROW_TILES)
+    weight_rows = spline_weight.rearrange("(m p) i g -> p m (i g)", p=P)
+
+    with ExitStack() as pools:
+        keep = pools.enter_context(tc.tile_pool(name="keep", bufs=1))
+        x_pool = pools.enter_context(tc.tile_pool(name="x_pool", bufs=2))
+        f32_pool = pools.enter_context(tc.tile_pool(name="f32_pool", bufs=3))
+        bf16_pool = pools.enter_context(tc.tile_pool(name="bf16_pool", bufs=2))
+        code_pool = pools.enter_context(tc.tile_pool(name="code_pool", bufs=4))
+        out_pool = pools.enter_context(tc.tile_pool(name="out_pool", bufs=4))
+        sum_banks = pools.enter_context(tc.psum_pool(name="sum_banks", bufs=TILES_PER_CHUNK))
+        work_banks = pools.enter_context(tc.psum_pool(name="work_banks", bufs=4))
+
+        ident_f32 = keep.tile([P, P], F32)
+        make_identity(nc, ident_f32[:])
+        ident_bf16 = keep.tile([P, P], BF16)
+        make_identity(nc, ident_bf16[:])
+        minus_one = keep.tile([P, 1], F32)
+        nc.vector.memset(minus_one[:], -1.0)
+
+        x_grouped = keep.tile([P, ROW_TILES * P * PACK], BF16, align_bytes=64)
+        x_codes = keep.tile([P, ROW_TILES * P], U32, align_bytes=64)
+        x_scales = keep.tile([P, ROW_TILES * P], U8, align_bytes=64)
+        weight_raw = keep.tile([P, OUT_BLOCKS, FEATURES * GRID], BF16)
+        weight_codes = keep.tile([P, GRID, OUTPUTS], U32, align_bytes=64)
+        weight_scales = keep.tile([P, GRID, OUTPUTS], U8, align_bytes=64)
+        w4_words = keep.tile([P, 2 * OUTPUTS], U8, align_bytes=64)
+        w4_scales = keep.tile([P, OUTPUTS], U8, align_bytes=64)
+        grid_rows = keep.tile([P, GRID], BF16)
+        minus_grid = keep.tile([P, GRID], F32)
+
+        nc.vector.memset(w4_scales[:].bitcast(I32), 0)
+
+        x_raw = {}
+
+        def load_x(chunk):
+            x_raw[chunk] = x_pool.tile([P, TILES_PER_CHUNK, FEATURES], BF16, name="x_raw")
+            first = chunk * TILES_PER_CHUNK
+            nc.sync.dma_start(out=x_raw[chunk][:], in_=x_rows[:, first : first + TILES_PER_CHUNK, :])
+
+        load_x(0)
+        nc.sync.dma_start(out=grid_rows[:], in_=grid_points.partition_broadcast(P))
+        nc.sync.dma_start(
+            out=w4_words[:].bitcast(I32), in_=base_activation_words.flatten_outer_dims().bitcast(I32)
+        )
+        w4_scale_rows = base_activation_scales.flatten_outer_dims()
+        for quadrant in range(4):
+            nc.sync.dma_start(
+                out=w4_scales[32 * quadrant : 32 * quadrant + 4, :].bitcast(I32),
+                in_=w4_scale_rows[4 * quadrant : 4 * quadrant + 4, :].bitcast(I32),
+            )
+        for m in range(OUT_BLOCKS):
+            nc.sync.dma_start(out=weight_raw[:, m, :], in_=weight_rows[:, m, :])
+        load_x(1)
+
+        nc.vector.tensor_scalar(
+            out=minus_grid[:], in0=grid_rows[:], scalar1=-1.0, scalar2=None, op0=ALU.mult
+        )
+
+        x_words = x_grouped[:].bitcast(F32).rearrange("p (n r u) -> p n r u", n=ROW_TILES, r=P, u=2)
+        base_tenth = {}
+
+        def prepare_x(chunk):
+            first = chunk * TILES_PER_CHUNK
+            for pair in range(TILES_PER_CHUNK // 2):
+                turned = work_banks.tile([P, 2, 2, P], F32, tag="bank")
+                for j in range(2):
+                    words = x_raw[chunk][:, 2 * pair + j, :].bitcast(F32)
+                    for u in range(2):
+                        nc.tensor.transpose(turned[:, j, u, :], words[:, u : FEATURES // 2 : 2], ident_f32[:])
+                n0 = first + 2 * pair
+                nc.scalar.copy(
+                    out=x_words[:, n0 : n0 + 2, :, :], in_=turned[:].rearrange("p j u r -> p j r u")
+                )
+            cols = slice(chunk * CHUNK_ROWS, (chunk + 1) * CHUNK_ROWS)
+            nc.vector.quantize_mx(
+                out=x_codes[:, cols].bitcast(FP8X4),
+                scales=x_scales[:, cols],
+                in_=x_grouped[:, chunk * CHUNK_COLS : (chunk + 1) * CHUNK_COLS],
+            )
+            base_tenth[chunk] = out_pool.tile([P, TILES_PER_CHUNK, OUTPUTS], F32, name="base_tenth", bufs=2)
+            for j in range(TILES_PER_CHUNK):
+                rows = slice((first + j) * P, (first + j + 1) * P)
+                base_sum = work_banks.tile([P, OUTPUTS], F32, tag="bank")
+                nc.tensor.matmul_mx(
+                    out=base_sum[:],
+                    lhsT=x_codes[:, rows].bitcast(FP8X4),
+                    lhsT_scale=x_scales[:, rows],
+                    rhs=w4_words[:].bitcast(FP4X4),
+                    rhs_scale=w4_scales[:],
+                    start=True,
+                    stop=True,
+                )
+                nc.scalar.mul(out=base_tenth[chunk][:, j, :], in_=base_sum[:], mul=0.1)
+
+        def prepare_weights(g):
+            grouped = bf16_pool.tile([P, OUTPUTS, PACK], BF16, name="weight_grouped", align_bytes=64)
+            for half in range(2):
+                turned = work_banks.tile([P, PACK, 2 * P], BF16, tag="bank")
+                for t in range(PACK):
+                    for j in range(2):
+                        nc.tensor.transpose(
+                            turned[:, t, j * P : (j + 1) * P],
+                            weight_raw[:, 2 * half + j, 8 * t + g : FEATURES * GRID : 8 * PACK],
+                            ident_bf16[:],
+                        )
+                nc.scalar.copy(
+                    out=grouped[:, half * 2 * P : (half + 1) * 2 * P, :],
+                    in_=turned[:].rearrange("p t o -> p o t"),
+                )
+            nc.vector.quantize_mx(
+                out=weight_codes[:, g, :].bitcast(FP8X4),
+                scales=weight_scales[:, g, :],
+                in_=grouped[:].rearrange("p o t -> p (o t)"),
+            )
+
+        basis = {}
+        basis_codes = {}
+        basis_scales = {}
+
+        def compute_basis(step):
+            chunk, g = divmod(step, GRID)
+            x_part = x_grouped[:, chunk * CHUNK_COLS : (chunk + 1) * CHUNK_COLS]
+            shift = minus_grid[:, g : g + 1]
+            dist = f32_pool.tile([P, CHUNK_COLS], F32, name="dist")
+            nc.scalar.activation(out=dist[:], in_=x_part, func=ACT.Abs, bias=shift, scale=1.0)
+            dist_sq = f32_pool.tile([P, CHUNK_COLS], F32, name="dist_sq")
+            nc.scalar.activation(out=dist_sq[:], in_=x_part, func=ACT.Square, bias=shift, scale=1.0)
+            gap_sq = f32_pool.tile([P, CHUNK_COLS], F32, name="gap_sq")
+            nc.scalar.activation(out=gap_sq[:], in_=dist[:], func=ACT.Square, bias=minus_one[:], scale=1.0)
+            nc.vector.scalar_tensor_tensor(
+                out=dist_sq[:], in0=dist[:], scalar=1.0, in1=dist_sq[:], op0=ALU.subtract, op1=ALU.mult
+            )
+            inner = bf16_pool.tile([P, CHUNK_COLS], BF16, name="inner")
+            nc.vector.tensor_scalar(
+                out=inner[:], in0=dist_sq[:], scalar1=-3.0, scalar2=-0.5, op0=ALU.mult, op1=ALU.add
+            )
+            outer = bf16_pool.tile([P, CHUNK_COLS], BF16, name="outer")
+            nc.vector.scalar_tensor_tensor(
+                out=outer[:], in0=dist[:], scalar=1.0, in1=gap_sq[:], op0=ALU.subtract, op1=ALU.mult
+            )
+            nc.vector.tensor_tensor(out=inner[:], in0=inner[:], in1=outer[:], op=ALU.max)
+            basis[step] = bf16_pool.tile([P, CHUNK_COLS], BF16, name="basis", align_bytes=64)
+            nc.vector.tensor_scalar(
+                out=basis[step][:], in0=inner[:], scalar1=-2.0, scalar2=0.0, op0=ALU.mult, op1=ALU.max
+            )
+
+        def quantise_basis(step):
+            basis_codes[step] = code_pool.tile([P, CHUNK_ROWS], U32, name="basis_codes", align_bytes=64)
+            basis_scales[step] = code_pool.tile([P, CHUNK_ROWS], U8, name="basis_scales", align_bytes=64)
+            nc.vector.quantize_mx(
+                out=basis_codes[step][:].bitcast(FP8X4), scales=basis_scales[step][:], in_=basis[step][:]
+            )
+
+        spline_sum = {}
+
+        def multiply(step):
+            chunk, g = divmod(step, GRID)
+            for j in range(TILES_PER_CHUNK):
+                if g == 0:
+                    spline_sum[j] = sum_banks.tile([P, OUTPUTS], F32, name="spline_sum")
+                rows = slice(j * P, (j + 1) * P)
+                nc.tensor.matmul_mx(
+                    out=spline_sum[j][:],
+                    lhsT=basis_codes[step][:, rows].bitcast(FP8X4),
+                    lhsT_scale=basis_scales[step][:, rows],
+                    rhs=weight_codes[:, g, :].bitcast(FP8X4),
+                    rhs_scale=weight_scales[:, g, :],
+                    start=(g == 0),
+                    stop=(g == GRID - 1),
+                )
+
+        def finish(chunk):
+            for j in range(TILES_PER_CHUNK):
+                result = out_pool.tile([P, OUTPUTS], F32, name="result")
+                nc.vector.tensor_tensor(
+                    out=result[:], in0=spline_sum[j][:], in1=base_tenth[chunk][:, j, :], op=ALU.add
+                )
+                nc.sync.dma_start(out=out_rows[:, chunk * TILES_PER_CHUNK + j, :], in_=result[:])
+
+        prepare_x(0)
+        for step in range(STEPS + 2):
+            if step < STEPS:
+                compute_basis(step)
+            if 1 <= step <= STEPS:
+                quantise_basis(step - 1)
+            if step >= 2:
+                chunk, g = divmod(step - 2, GRID)
+                if chunk == 0:
+                    prepare_weights(g)
+                multiply(step - 2)
+                if g == GRID - 1:
+                    finish(chunk)
+                if g == GRID // 2 and chunk + 1 < CHUNKS:
+                    prepare_x(chunk + 1)
+                    if chunk + 2 < CHUNKS:
+                        load_x(chunk + 2)

@@ -23,6 +23,7 @@ CHUNK_ROWS = TILES_PER_CHUNK * P
 CHUNK_COLS = CHUNK_ROWS * PACK
 STEPS = CHUNKS * GRID
 OUT_BLOCKS = OUTPUTS // P
+SCALAR_COLS = 640
 
 FLOPS = 2 * BATCH * OUTPUTS * (FEATURES * GRID + FEATURES)
 
@@ -51,6 +52,8 @@ def tile_advancedkanlayer_pa_kernel(
         make_identity(nc, ident_bf16[:])
         minus_one = keep.tile([P, 1], F32)
         nc.vector.memset(minus_one[:], -1.0)
+        minus_half = keep.tile([P, 1], F32)
+        nc.vector.memset(minus_half[:], -0.5)
 
         x_grouped = keep.tile([P, ROW_TILES * P * PACK], BF16, align_bytes=64)
         x_codes = keep.tile([P, ROW_TILES * P], U32, align_bytes=64)
@@ -166,8 +169,22 @@ def tile_advancedkanlayer_pa_kernel(
                 out=dist_sq[:], in0=dist[:], scalar=1.0, in1=dist_sq[:], op0=ALU.subtract, op1=ALU.mult
             )
             inner = bf16_pool.tile([P, CHUNK_COLS], BF16, name="inner")
+            scalar_cols = SCALAR_COLS if chunk > 0 else 0
+            if scalar_cols > 0:
+                nc.scalar.activation(
+                    out=inner[:, :scalar_cols],
+                    in_=dist_sq[:, :scalar_cols],
+                    func=ACT.Identity,
+                    bias=minus_half[:],
+                    scale=-3.0,
+                )
             nc.vector.tensor_scalar(
-                out=inner[:], in0=dist_sq[:], scalar1=-3.0, scalar2=-0.5, op0=ALU.mult, op1=ALU.add
+                out=inner[:, scalar_cols:],
+                in0=dist_sq[:, scalar_cols:],
+                scalar1=-3.0,
+                scalar2=-0.5,
+                op0=ALU.mult,
+                op1=ALU.add,
             )
             outer = bf16_pool.tile([P, CHUNK_COLS], BF16, name="outer")
             nc.vector.scalar_tensor_tensor(

@@ -45,6 +45,7 @@ def tile_advancedkanlayer_pa_kernel(
         out_pool = pools.enter_context(tc.tile_pool(name="out_pool", bufs=4))
         sum_banks = pools.enter_context(tc.psum_pool(name="sum_banks", bufs=TILES_PER_CHUNK))
         work_banks = pools.enter_context(tc.psum_pool(name="work_banks", bufs=4))
+        pools.enter_context(tc.manual_schedule())
 
         ident_f32 = keep.tile([P, P], F32)
         make_identity(nc, ident_f32[:])
@@ -77,6 +78,8 @@ def tile_advancedkanlayer_pa_kernel(
 
         load_x(0)
         nc.sync.dma_start(out=grid_rows[:], in_=grid_points.partition_broadcast(P))
+        for m in range(OUT_BLOCKS):
+            nc.sync.dma_start(out=weight_raw[:, m, :], in_=weight_rows[:, m, :])
         nc.sync.dma_start(
             out=w4_words[:].bitcast(I32), in_=base_activation_words.flatten_outer_dims().bitcast(I32)
         )
@@ -86,8 +89,6 @@ def tile_advancedkanlayer_pa_kernel(
                 out=w4_scales[32 * quadrant : 32 * quadrant + 4, :].bitcast(I32),
                 in_=w4_scale_rows[4 * quadrant : 4 * quadrant + 4, :].bitcast(I32),
             )
-        for m in range(OUT_BLOCKS):
-            nc.sync.dma_start(out=weight_raw[:, m, :], in_=weight_rows[:, m, :])
         load_x(1)
 
         nc.vector.tensor_scalar(
@@ -97,27 +98,31 @@ def tile_advancedkanlayer_pa_kernel(
         x_words = x_grouped[:].bitcast(F32).rearrange("p (n r u) -> p n r u", n=ROW_TILES, r=P, u=2)
         base_tenth = {}
 
-        def prepare_x(chunk):
-            first = chunk * TILES_PER_CHUNK
+        def turn_x(chunk):
             for pair in range(TILES_PER_CHUNK // 2):
                 turned = work_banks.tile([P, 2, 2, P], F32, tag="bank")
                 for j in range(2):
                     words = x_raw[chunk][:, 2 * pair + j, :].bitcast(F32)
                     for u in range(2):
                         nc.tensor.transpose(turned[:, j, u, :], words[:, u : FEATURES // 2 : 2], ident_f32[:])
-                n0 = first + 2 * pair
+                n0 = chunk * TILES_PER_CHUNK + 2 * pair
                 nc.scalar.copy(
                     out=x_words[:, n0 : n0 + 2, :, :], in_=turned[:].rearrange("p j u r -> p j r u")
                 )
+
+        def quantise_x(chunk):
             cols = slice(chunk * CHUNK_ROWS, (chunk + 1) * CHUNK_ROWS)
             nc.vector.quantize_mx(
                 out=x_codes[:, cols].bitcast(FP8X4),
                 scales=x_scales[:, cols],
                 in_=x_grouped[:, chunk * CHUNK_COLS : (chunk + 1) * CHUNK_COLS],
             )
+
+        def base_product(chunk):
             base_tenth[chunk] = out_pool.tile([P, TILES_PER_CHUNK, OUTPUTS], F32, name="base_tenth", bufs=2)
             for j in range(TILES_PER_CHUNK):
-                rows = slice((first + j) * P, (first + j + 1) * P)
+                n = chunk * TILES_PER_CHUNK + j
+                rows = slice(n * P, (n + 1) * P)
                 base_sum = work_banks.tile([P, OUTPUTS], F32, tag="bank")
                 nc.tensor.matmul_mx(
                     out=base_sum[:],
@@ -130,8 +135,10 @@ def tile_advancedkanlayer_pa_kernel(
                 )
                 nc.scalar.mul(out=base_tenth[chunk][:, j, :], in_=base_sum[:], mul=0.1)
 
-        def prepare_weights(g):
-            grouped = bf16_pool.tile([P, OUTPUTS, PACK], BF16, name="weight_grouped", align_bytes=64)
+        weight_grouped = {}
+
+        def turn_weights(g):
+            weight_grouped[g] = bf16_pool.tile([P, OUTPUTS, PACK], BF16, name="weight_grouped", align_bytes=64)
             for half in range(2):
                 turned = work_banks.tile([P, PACK, 2 * P], BF16, tag="bank")
                 for t in range(PACK):
@@ -142,58 +149,80 @@ def tile_advancedkanlayer_pa_kernel(
                             ident_bf16[:],
                         )
                 nc.scalar.copy(
-                    out=grouped[:, half * 2 * P : (half + 1) * 2 * P, :],
+                    out=weight_grouped[g][:, half * 2 * P : (half + 1) * 2 * P, :],
                     in_=turned[:].rearrange("p t o -> p o t"),
                 )
+
+        def quantise_weights(g):
             nc.vector.quantize_mx(
                 out=weight_codes[:, g, :].bitcast(FP8X4),
                 scales=weight_scales[:, g, :],
-                in_=grouped[:].rearrange("p o t -> p (o t)"),
+                in_=weight_grouped[g][:].rearrange("p o t -> p (o t)"),
             )
 
-        basis = {}
-        basis_codes = {}
-        basis_scales = {}
+        dist, dist_sq, gap_sq, inner, outer, basis, basis_codes, basis_scales = {}, {}, {}, {}, {}, {}, {}, {}
 
-        def compute_basis(step):
+        def squares(step):
             chunk, g = divmod(step, GRID)
             x_part = x_grouped[:, chunk * CHUNK_COLS : (chunk + 1) * CHUNK_COLS]
             shift = minus_grid[:, g : g + 1]
-            dist = f32_pool.tile([P, CHUNK_COLS], F32, name="dist")
-            nc.scalar.activation(out=dist[:], in_=x_part, func=ACT.Abs, bias=shift, scale=1.0)
-            dist_sq = f32_pool.tile([P, CHUNK_COLS], F32, name="dist_sq")
-            nc.scalar.activation(out=dist_sq[:], in_=x_part, func=ACT.Square, bias=shift, scale=1.0)
-            gap_sq = f32_pool.tile([P, CHUNK_COLS], F32, name="gap_sq")
-            nc.scalar.activation(out=gap_sq[:], in_=dist[:], func=ACT.Square, bias=minus_one[:], scale=1.0)
-            nc.vector.scalar_tensor_tensor(
-                out=dist_sq[:], in0=dist[:], scalar=1.0, in1=dist_sq[:], op0=ALU.subtract, op1=ALU.mult
+            dist[step] = f32_pool.tile([P, CHUNK_COLS], F32, name="dist")
+            nc.scalar.activation(out=dist[step][:], in_=x_part, func=ACT.Abs, bias=shift, scale=1.0)
+            dist_sq[step] = f32_pool.tile([P, CHUNK_COLS], F32, name="dist_sq")
+            nc.scalar.activation(out=dist_sq[step][:], in_=x_part, func=ACT.Square, bias=shift, scale=1.0)
+            gap_sq[step] = f32_pool.tile([P, CHUNK_COLS], F32, name="gap_sq")
+            nc.scalar.activation(
+                out=gap_sq[step][:], in_=dist[step][:], func=ACT.Square, bias=minus_one[:], scale=1.0
             )
-            inner = bf16_pool.tile([P, CHUNK_COLS], BF16, name="inner")
-            scalar_cols = SCALAR_COLS if chunk > 0 else 0
+
+        def inner_product(step):
+            nc.vector.scalar_tensor_tensor(
+                out=dist_sq[step][:],
+                in0=dist[step][:],
+                scalar=1.0,
+                in1=dist_sq[step][:],
+                op0=ALU.subtract,
+                op1=ALU.mult,
+            )
+
+        def inner_finish(step):
+            inner[step] = bf16_pool.tile([P, CHUNK_COLS], BF16, name="inner")
+            scalar_cols = SCALAR_COLS if step >= GRID else 0
             if scalar_cols > 0:
                 nc.scalar.activation(
-                    out=inner[:, :scalar_cols],
-                    in_=dist_sq[:, :scalar_cols],
+                    out=inner[step][:, :scalar_cols],
+                    in_=dist_sq[step][:, :scalar_cols],
                     func=ACT.Identity,
                     bias=minus_half[:],
                     scale=-3.0,
                 )
             nc.vector.tensor_scalar(
-                out=inner[:, scalar_cols:],
-                in0=dist_sq[:, scalar_cols:],
+                out=inner[step][:, scalar_cols:],
+                in0=dist_sq[step][:, scalar_cols:],
                 scalar1=-3.0,
                 scalar2=-0.5,
                 op0=ALU.mult,
                 op1=ALU.add,
             )
-            outer = bf16_pool.tile([P, CHUNK_COLS], BF16, name="outer")
+
+        def outer_cubic(step):
+            outer[step] = bf16_pool.tile([P, CHUNK_COLS], BF16, name="outer")
             nc.vector.scalar_tensor_tensor(
-                out=outer[:], in0=dist[:], scalar=1.0, in1=gap_sq[:], op0=ALU.subtract, op1=ALU.mult
+                out=outer[step][:],
+                in0=dist[step][:],
+                scalar=1.0,
+                in1=gap_sq[step][:],
+                op0=ALU.subtract,
+                op1=ALU.mult,
             )
-            nc.vector.tensor_tensor(out=inner[:], in0=inner[:], in1=outer[:], op=ALU.max)
+
+        def pick(step):
+            nc.vector.tensor_tensor(out=inner[step][:], in0=inner[step][:], in1=outer[step][:], op=ALU.max)
+
+        def to_basis(step):
             basis[step] = bf16_pool.tile([P, CHUNK_COLS], BF16, name="basis", align_bytes=64)
             nc.vector.tensor_scalar(
-                out=basis[step][:], in0=inner[:], scalar1=-2.0, scalar2=0.0, op0=ALU.mult, op1=ALU.max
+                out=basis[step][:], in0=inner[step][:], scalar1=-2.0, scalar2=0.0, op0=ALU.mult, op1=ALU.max
             )
 
         def quantise_basis(step):
@@ -229,20 +258,39 @@ def tile_advancedkanlayer_pa_kernel(
                 )
                 nc.sync.dma_start(out=out_rows[:, chunk * TILES_PER_CHUNK + j, :], in_=result[:])
 
-        prepare_x(0)
-        for step in range(STEPS + 2):
-            if step < STEPS:
-                compute_basis(step)
-            if 1 <= step <= STEPS:
-                quantise_basis(step - 1)
-            if step >= 2:
-                chunk, g = divmod(step - 2, GRID)
-                if chunk == 0:
-                    prepare_weights(g)
-                multiply(step - 2)
-                if g == GRID - 1:
-                    finish(chunk)
-                if g == GRID // 2 and chunk + 1 < CHUNKS:
-                    prepare_x(chunk + 1)
-                    if chunk + 2 < CHUNKS:
-                        load_x(chunk + 2)
+        def is_step(step):
+            return 0 <= step < STEPS
+
+        turn_x(0)
+        for r in range(STEPS + 5):
+            chunk, g = divmod(r, GRID)
+            if is_step(r):
+                squares(r)
+            if r - 4 >= 0 and (r - 4) % GRID == GRID - 1:
+                finish((r - 4) // GRID)
+            if is_step(r - 1):
+                inner_product(r - 1)
+            if is_step(r - 2):
+                pick(r - 2)
+            if is_step(r - 1):
+                outer_cubic(r - 1)
+            if is_step(r - 2):
+                to_basis(r - 2)
+            if is_step(r - 1):
+                inner_finish(r - 1)
+            if is_step(r - 2):
+                quantise_basis(r - 2)
+            if 0 <= r - 2 < GRID:
+                quantise_weights(r - 2)
+            if 0 <= r - 1 < GRID:
+                turn_weights(r - 1)
+            if is_step(r - 3):
+                multiply(r - 3)
+            if is_step(r) and g == 1:
+                quantise_x(chunk)
+            if is_step(r) and g == 2:
+                base_product(chunk)
+            if g == GRID - 3 and chunk + 1 < CHUNKS:
+                turn_x(chunk + 1)
+                if chunk + 2 < CHUNKS:
+                    load_x(chunk + 2)

@@ -24,6 +24,7 @@ CHUNK_COLS = CHUNK_ROWS * PACK
 STEPS = CHUNKS * GRID
 OUT_BLOCKS = OUTPUTS // P
 SCALAR_COLS = 640
+SCALAR_COLS_AT_ENDS = 1664
 
 FLOPS = 2 * BATCH * OUTPUTS * (FEATURES * GRID + FEATURES)
 
@@ -66,6 +67,8 @@ def tile_advancedkanlayer_pa_kernel(
         w4_scales = keep.tile([P, OUTPUTS], U8, align_bytes=64)
         grid_rows = keep.tile([P, GRID], BF16)
         minus_grid = keep.tile([P, GRID], F32)
+        shift = keep.tile([P, GRID], F32)
+        twice_grid = keep.tile([P, GRID], F32)
 
         nc.vector.memset(w4_scales[:].bitcast(I32), 0)
 
@@ -93,6 +96,27 @@ def tile_advancedkanlayer_pa_kernel(
 
         nc.vector.tensor_scalar(
             out=minus_grid[:], in0=grid_rows[:], scalar1=-1.0, scalar2=None, op0=ALU.mult
+        )
+        nc.vector.tensor_scalar(
+            out=shift[:, 0:1], in0=grid_rows[:, 0:1], scalar1=-1.0, scalar2=-1.0, op0=ALU.mult, op1=ALU.add
+        )
+        nc.vector.tensor_scalar(
+            out=shift[:, GRID - 1 : GRID],
+            in0=grid_rows[:, GRID - 1 : GRID],
+            scalar1=1.0,
+            scalar2=-1.0,
+            op0=ALU.mult,
+            op1=ALU.add,
+        )
+        nc.vector.tensor_scalar(
+            out=twice_grid[:, 0:1], in0=grid_rows[:, 0:1], scalar1=2.0, scalar2=None, op0=ALU.mult
+        )
+        nc.vector.tensor_scalar(
+            out=twice_grid[:, GRID - 1 : GRID],
+            in0=grid_rows[:, GRID - 1 : GRID],
+            scalar1=-2.0,
+            scalar2=None,
+            op0=ALU.mult,
         )
 
         x_words = x_grouped[:].bitcast(F32).rearrange("p (n r u) -> p n r u", n=ROW_TILES, r=P, u=2)
@@ -162,32 +186,61 @@ def tile_advancedkanlayer_pa_kernel(
 
         dist, dist_sq, gap_sq, inner, outer, basis, basis_codes, basis_scales = {}, {}, {}, {}, {}, {}, {}, {}
 
+        def is_end(step):
+            return step % GRID in (0, GRID - 1)
+
+        def to_gap(step):
+            g = step % GRID
+            return shift[:, g : g + 1] if is_end(step) else -1.0
+
+        def end_distance(step):
+            chunk, g = divmod(step, GRID)
+            x_part = x_grouped[:, chunk * CHUNK_COLS : (chunk + 1) * CHUNK_COLS]
+            sign = 1.0 if g == 0 else -1.0
+            double = bf16_pool.tile([P, CHUNK_COLS], BF16, name="double")
+            nc.vector.tensor_scalar(
+                out=double[:], in0=x_part, scalar1=2.0 * sign, scalar2=None, op0=ALU.mult
+            )
+            dist[step] = f32_pool.tile([P, CHUNK_COLS], F32, name="dist")
+            nc.vector.scalar_tensor_tensor(
+                out=dist[step][:],
+                in0=double[:],
+                scalar=twice_grid[:, g : g + 1],
+                in1=x_part,
+                op0=ALU.max,
+                op1=ALU.subtract if g == 0 else ALU.add,
+            )
+
         def squares(step):
             chunk, g = divmod(step, GRID)
             x_part = x_grouped[:, chunk * CHUNK_COLS : (chunk + 1) * CHUNK_COLS]
-            shift = minus_grid[:, g : g + 1]
-            dist[step] = f32_pool.tile([P, CHUNK_COLS], F32, name="dist")
-            nc.scalar.activation(out=dist[step][:], in_=x_part, func=ACT.Abs, bias=shift, scale=1.0)
+            minus_g = minus_grid[:, g : g + 1]
+            if not is_end(step):
+                dist[step] = f32_pool.tile([P, CHUNK_COLS], F32, name="dist")
+                nc.scalar.activation(out=dist[step][:], in_=x_part, func=ACT.Abs, bias=minus_g, scale=1.0)
             dist_sq[step] = f32_pool.tile([P, CHUNK_COLS], F32, name="dist_sq")
-            nc.scalar.activation(out=dist_sq[step][:], in_=x_part, func=ACT.Square, bias=shift, scale=1.0)
+            nc.scalar.activation(out=dist_sq[step][:], in_=x_part, func=ACT.Square, bias=minus_g, scale=1.0)
             gap_sq[step] = f32_pool.tile([P, CHUNK_COLS], F32, name="gap_sq")
+            gap_bias = shift[:, g : g + 1] if is_end(step) else minus_one[:]
             nc.scalar.activation(
-                out=gap_sq[step][:], in_=dist[step][:], func=ACT.Square, bias=minus_one[:], scale=1.0
+                out=gap_sq[step][:], in_=dist[step][:], func=ACT.Square, bias=gap_bias, scale=1.0
             )
 
         def inner_product(step):
             nc.vector.scalar_tensor_tensor(
                 out=dist_sq[step][:],
                 in0=dist[step][:],
-                scalar=1.0,
+                scalar=to_gap(step),
                 in1=dist_sq[step][:],
-                op0=ALU.subtract,
+                op0=ALU.add,
                 op1=ALU.mult,
             )
 
         def inner_finish(step):
             inner[step] = bf16_pool.tile([P, CHUNK_COLS], BF16, name="inner")
-            scalar_cols = SCALAR_COLS if step >= GRID else 0
+            scalar_cols = SCALAR_COLS_AT_ENDS if is_end(step) else SCALAR_COLS
+            if step < GRID:
+                scalar_cols = 0
             if scalar_cols > 0:
                 nc.scalar.activation(
                     out=inner[step][:, :scalar_cols],
@@ -210,9 +263,9 @@ def tile_advancedkanlayer_pa_kernel(
             nc.vector.scalar_tensor_tensor(
                 out=outer[step][:],
                 in0=dist[step][:],
-                scalar=1.0,
+                scalar=to_gap(step),
                 in1=gap_sq[step][:],
-                op0=ALU.subtract,
+                op0=ALU.add,
                 op1=ALU.mult,
             )
 
@@ -262,6 +315,7 @@ def tile_advancedkanlayer_pa_kernel(
             return 0 <= step < STEPS
 
         turn_x(0)
+        end_distance(0)
         for r in range(STEPS + 5):
             chunk, g = divmod(r, GRID)
             if is_step(r):
@@ -282,6 +336,8 @@ def tile_advancedkanlayer_pa_kernel(
                 quantise_basis(r - 2)
             if 0 <= r - 2 < GRID:
                 quantise_weights(r - 2)
+            if is_step(r + 1) and is_end(r + 1):
+                end_distance(r + 1)
             if 0 <= r - 1 < GRID:
                 turn_weights(r - 1)
             if is_step(r - 3):

@@ -17,14 +17,17 @@ P = 128
 PACK = 4
 BATCH, FEATURES, OUTPUTS, GRID = 2048, 512, 512, 8
 ROW_TILES = BATCH // P
-TILES_PER_CHUNK = 4
-CHUNKS = ROW_TILES // TILES_PER_CHUNK
-CHUNK_ROWS = TILES_PER_CHUNK * P
-CHUNK_COLS = CHUNK_ROWS * PACK
-STEPS = CHUNKS * GRID
+TILES = 2
+CHUNKS = ROW_TILES // TILES
+ROWS = TILES * P
+KNOTS = 2
+STEPS_PER_CHUNK = GRID // KNOTS
+STEPS = CHUNKS * STEPS_PER_CHUNK
+BANK = P * PACK
+KNOT_COLS = TILES * BANK
+STEP_COLS = KNOTS * KNOT_COLS
+BANKS = KNOTS * TILES
 OUT_BLOCKS = OUTPUTS // P
-SCALAR_COLS = 640
-SCALAR_COLS_AT_ENDS = 1664
 
 FLOPS = 2 * BATCH * OUTPUTS * (FEATURES * GRID + FEATURES)
 
@@ -39,27 +42,23 @@ def tile_advancedkanlayer_pa_kernel(
 
     with ExitStack() as pools:
         keep = pools.enter_context(tc.tile_pool(name="keep", bufs=1))
-        x_pool = pools.enter_context(tc.tile_pool(name="x_pool", bufs=2))
+        x_pool = pools.enter_context(tc.tile_pool(name="x_pool", bufs=3))
         f32_pool = pools.enter_context(tc.tile_pool(name="f32_pool", bufs=3))
         bf16_pool = pools.enter_context(tc.tile_pool(name="bf16_pool", bufs=2))
-        code_pool = pools.enter_context(tc.tile_pool(name="code_pool", bufs=4))
-        out_pool = pools.enter_context(tc.tile_pool(name="out_pool", bufs=4))
-        sum_banks = pools.enter_context(tc.psum_pool(name="sum_banks", bufs=TILES_PER_CHUNK))
-        work_banks = pools.enter_context(tc.psum_pool(name="work_banks", bufs=4))
+        code_pool = pools.enter_context(tc.tile_pool(name="code_pool", bufs=3))
+        out_pool = pools.enter_context(tc.tile_pool(name="out_pool", bufs=2))
+        sum_banks = pools.enter_context(tc.psum_pool(name="sum_banks", bufs=TILES))
+        dist_banks = pools.enter_context(tc.psum_pool(name="dist_banks", bufs=BANKS))
+        work_banks = pools.enter_context(tc.psum_pool(name="work_banks", bufs=2))
         pools.enter_context(tc.manual_schedule())
 
         ident_f32 = keep.tile([P, P], F32)
         make_identity(nc, ident_f32[:])
         ident_bf16 = keep.tile([P, P], BF16)
         make_identity(nc, ident_bf16[:])
-        minus_one = keep.tile([P, 1], F32)
-        nc.vector.memset(minus_one[:], -1.0)
-        minus_half = keep.tile([P, 1], F32)
-        nc.vector.memset(minus_half[:], -0.5)
+        minus_ident = keep.tile([P, P], BF16)
+        nc.vector.tensor_scalar(out=minus_ident[:], in0=ident_bf16[:], scalar1=-1.0, scalar2=None, op0=ALU.mult)
 
-        x_grouped = keep.tile([P, ROW_TILES * P * PACK], BF16, align_bytes=64)
-        x_codes = keep.tile([P, ROW_TILES * P], U32, align_bytes=64)
-        x_scales = keep.tile([P, ROW_TILES * P], U8, align_bytes=64)
         weight_raw = keep.tile([P, OUT_BLOCKS, FEATURES * GRID], BF16)
         weight_codes = keep.tile([P, GRID, OUTPUTS], U32, align_bytes=64)
         weight_scales = keep.tile([P, GRID, OUTPUTS], U8, align_bytes=64)
@@ -68,21 +67,23 @@ def tile_advancedkanlayer_pa_kernel(
         grid_rows = keep.tile([P, GRID], BF16)
         minus_grid = keep.tile([P, GRID], F32)
         shift = keep.tile([P, GRID], F32)
-        twice_grid = keep.tile([P, GRID], F32)
+        fold_bias = keep.tile([P, GRID], F32)
 
         nc.vector.memset(w4_scales[:].bitcast(I32), 0)
+        nc.vector.memset(shift[:], -1.0)
 
         x_raw = {}
 
         def load_x(chunk):
-            x_raw[chunk] = x_pool.tile([P, TILES_PER_CHUNK, FEATURES], BF16, name="x_raw")
-            first = chunk * TILES_PER_CHUNK
-            nc.sync.dma_start(out=x_raw[chunk][:], in_=x_rows[:, first : first + TILES_PER_CHUNK, :])
+            x_raw[chunk] = x_pool.tile([P, TILES, FEATURES], BF16, name="x_raw")
+            first = chunk * TILES
+            nc.sync.dma_start(out=x_raw[chunk][:], in_=x_rows[:, first : first + TILES, :])
 
         load_x(0)
         nc.sync.dma_start(out=grid_rows[:], in_=grid_points.partition_broadcast(P))
         for m in range(OUT_BLOCKS):
             nc.sync.dma_start(out=weight_raw[:, m, :], in_=weight_rows[:, m, :])
+        load_x(1)
         nc.sync.dma_start(
             out=w4_words[:].bitcast(I32), in_=base_activation_words.flatten_outer_dims().bitcast(I32)
         )
@@ -92,72 +93,66 @@ def tile_advancedkanlayer_pa_kernel(
                 out=w4_scales[32 * quadrant : 32 * quadrant + 4, :].bitcast(I32),
                 in_=w4_scale_rows[4 * quadrant : 4 * quadrant + 4, :].bitcast(I32),
             )
-        load_x(1)
 
+        LOW, HIGH = 0, GRID - 1
         nc.vector.tensor_scalar(
             out=minus_grid[:], in0=grid_rows[:], scalar1=-1.0, scalar2=None, op0=ALU.mult
         )
-        nc.vector.tensor_scalar(
-            out=shift[:, 0:1], in0=grid_rows[:, 0:1], scalar1=-1.0, scalar2=-1.0, op0=ALU.mult, op1=ALU.add
-        )
-        nc.vector.tensor_scalar(
-            out=shift[:, GRID - 1 : GRID],
-            in0=grid_rows[:, GRID - 1 : GRID],
-            scalar1=1.0,
-            scalar2=-1.0,
-            op0=ALU.mult,
-            op1=ALU.add,
-        )
-        nc.vector.tensor_scalar(
-            out=twice_grid[:, 0:1], in0=grid_rows[:, 0:1], scalar1=2.0, scalar2=None, op0=ALU.mult
-        )
-        nc.vector.tensor_scalar(
-            out=twice_grid[:, GRID - 1 : GRID],
-            in0=grid_rows[:, GRID - 1 : GRID],
-            scalar1=-2.0,
-            scalar2=None,
-            op0=ALU.mult,
-        )
+        for g, sign in ((LOW, -1.0), (HIGH, 1.0)):
+            nc.vector.tensor_scalar(
+                out=shift[:, g : g + 1],
+                in0=grid_rows[:, g : g + 1],
+                scalar1=sign,
+                scalar2=-1.0,
+                op0=ALU.mult,
+                op1=ALU.add,
+            )
+            nc.vector.tensor_scalar(
+                out=fold_bias[:, g : g + 1],
+                in0=grid_rows[:, g : g + 1],
+                scalar1=-2.0 * sign,
+                scalar2=None,
+                op0=ALU.mult,
+            )
 
-        x_words = x_grouped[:].bitcast(F32).rearrange("p (n r u) -> p n r u", n=ROW_TILES, r=P, u=2)
-        base_tenth = {}
+        x_grouped, x_codes, x_scales, base_tenth = {}, {}, {}, {}
 
         def turn_x(chunk):
-            for pair in range(TILES_PER_CHUNK // 2):
-                turned = work_banks.tile([P, 2, 2, P], F32, tag="bank")
-                for j in range(2):
-                    words = x_raw[chunk][:, 2 * pair + j, :].bitcast(F32)
-                    for u in range(2):
-                        nc.tensor.transpose(turned[:, j, u, :], words[:, u : FEATURES // 2 : 2], ident_f32[:])
-                n0 = chunk * TILES_PER_CHUNK + 2 * pair
-                nc.scalar.copy(
-                    out=x_words[:, n0 : n0 + 2, :, :], in_=turned[:].rearrange("p j u r -> p j r u")
-                )
+            turned = work_banks.tile([P, TILES, 2, P], F32, tag="bank")
+            for j in range(TILES):
+                words = x_raw[chunk][:, j, :].bitcast(F32)
+                for u in range(2):
+                    nc.tensor.transpose(turned[:, j, u, :], words[:, u : FEATURES // 2 : 2], ident_f32[:])
+            x_grouped[chunk] = x_pool.tile([P, KNOT_COLS], BF16, name="x_grouped", align_bytes=64)
+            nc.scalar.copy(
+                out=x_grouped[chunk][:].bitcast(F32).rearrange("p (j r u) -> p j r u", j=TILES, u=2),
+                in_=turned[:].rearrange("p j u r -> p j r u"),
+            )
 
         def quantise_x(chunk):
-            cols = slice(chunk * CHUNK_ROWS, (chunk + 1) * CHUNK_ROWS)
+            x_codes[chunk] = code_pool.tile([P, ROWS], U32, name="x_codes", align_bytes=64)
+            x_scales[chunk] = code_pool.tile([P, ROWS], U8, name="x_scales", align_bytes=64)
             nc.vector.quantize_mx(
-                out=x_codes[:, cols].bitcast(FP8X4),
-                scales=x_scales[:, cols],
-                in_=x_grouped[:, chunk * CHUNK_COLS : (chunk + 1) * CHUNK_COLS],
+                out=x_codes[chunk][:].bitcast(FP8X4), scales=x_scales[chunk][:], in_=x_grouped[chunk][:]
             )
 
         def base_product(chunk):
-            base_tenth[chunk] = out_pool.tile([P, TILES_PER_CHUNK, OUTPUTS], F32, name="base_tenth", bufs=2)
-            for j in range(TILES_PER_CHUNK):
-                n = chunk * TILES_PER_CHUNK + j
-                rows = slice(n * P, (n + 1) * P)
+            base_tenth[chunk] = out_pool.tile([P, TILES, OUTPUTS], F32, name="base_tenth")
+            for j in range(TILES):
+                rows = slice(j * P, (j + 1) * P)
                 base_sum = work_banks.tile([P, OUTPUTS], F32, tag="bank")
                 nc.tensor.matmul_mx(
                     out=base_sum[:],
-                    lhsT=x_codes[:, rows].bitcast(FP8X4),
-                    lhsT_scale=x_scales[:, rows],
+                    lhsT=x_codes[chunk][:, rows].bitcast(FP8X4),
+                    lhsT_scale=x_scales[chunk][:, rows],
                     rhs=w4_words[:].bitcast(FP4X4),
                     rhs_scale=w4_scales[:],
                     start=True,
                     stop=True,
                 )
-                nc.scalar.mul(out=base_tenth[chunk][:, j, :], in_=base_sum[:], mul=0.1)
+                nc.vector.tensor_scalar(
+                    out=base_tenth[chunk][:, j, :], in0=base_sum[:], scalar1=0.1, scalar2=None, op0=ALU.mult
+                )
 
         weight_grouped = {}
 
@@ -184,74 +179,108 @@ def tile_advancedkanlayer_pa_kernel(
                 in_=weight_grouped[g][:].rearrange("p o t -> p (o t)"),
             )
 
-        dist, dist_sq, gap_sq, inner, outer, basis, basis_codes, basis_scales = {}, {}, {}, {}, {}, {}, {}, {}
+        folded, dist, dist_sq, gap_sq = {}, {}, {}, {}
+        inner, outer, basis, basis_codes, basis_scales = {}, {}, {}, {}, {}
 
-        def is_end(step):
-            return step % GRID in (0, GRID - 1)
+        def knots_of(step):
+            chunk, pair = divmod(step, STEPS_PER_CHUNK)
+            return chunk, [pair * KNOTS + i for i in range(KNOTS)]
 
-        def to_gap(step):
-            g = step % GRID
-            return shift[:, g : g + 1] if is_end(step) else -1.0
+        def bank_cols(i, j):
+            first = i * KNOT_COLS + j * BANK
+            return slice(first, first + BANK)
 
-        def end_distance(step):
-            chunk, g = divmod(step, GRID)
-            x_part = x_grouped[:, chunk * CHUNK_COLS : (chunk + 1) * CHUNK_COLS]
-            sign = 1.0 if g == 0 else -1.0
-            double = bf16_pool.tile([P, CHUNK_COLS], BF16, name="double")
-            nc.vector.tensor_scalar(
-                out=double[:], in0=x_part, scalar1=2.0 * sign, scalar2=None, op0=ALU.mult
-            )
-            dist[step] = f32_pool.tile([P, CHUNK_COLS], F32, name="dist")
-            nc.vector.scalar_tensor_tensor(
-                out=dist[step][:],
-                in0=double[:],
-                scalar=twice_grid[:, g : g + 1],
-                in1=x_part,
-                op0=ALU.max,
-                op1=ALU.subtract if g == 0 else ALU.add,
-            )
+        def fold(step):
+            chunk, knots = knots_of(step)
+            folded[step] = f32_pool.tile([P, KNOTS, TILES, FEATURES], F32, name="folded", bufs=2)
+            for i, g in enumerate(knots):
+                if g == LOW:
+                    func, bias, scale = ACT.Relu, fold_bias[:, g : g + 1], -2.0
+                elif g == HIGH:
+                    func, bias, scale = ACT.Relu, fold_bias[:, g : g + 1], 2.0
+                else:
+                    func, bias, scale = ACT.Abs, minus_grid[:, g : g + 1], 1.0
+                nc.scalar.activation(
+                    out=folded[step][:, i, :, :], in_=x_raw[chunk][:], func=func, bias=bias, scale=scale
+                )
+
+        def turn_dist(step):
+            chunk, knots = knots_of(step)
+            for i, g in enumerate(knots):
+                for j in range(TILES):
+                    bank = dist_banks.tile([P, PACK, P], F32, name="dist")
+                    for t in range(PACK):
+                        if g in (LOW, HIGH):
+                            nc.tensor.matmul(
+                                bank[:, t, :],
+                                lhsT=x_raw[chunk][:, j, t:FEATURES:PACK],
+                                rhs=ident_bf16[:] if g == LOW else minus_ident[:],
+                                start=True,
+                                stop=False,
+                            )
+                        nc.tensor.matmul(
+                            bank[:, t, :],
+                            lhsT=folded[step][:, i, j, t:FEATURES:PACK],
+                            rhs=ident_f32[:],
+                            start=g not in (LOW, HIGH),
+                            stop=True,
+                            is_transpose=True,
+                        )
+                    dist[step, i, j] = bank
+
+        def rows_first(bank):
+            return bank[:].rearrange("p t r -> p r t")
+
+        def by_row(tile_cols):
+            return tile_cols.rearrange("p (r t) -> p r t", t=PACK)
 
         def squares(step):
-            chunk, g = divmod(step, GRID)
-            x_part = x_grouped[:, chunk * CHUNK_COLS : (chunk + 1) * CHUNK_COLS]
-            minus_g = minus_grid[:, g : g + 1]
-            if not is_end(step):
-                dist[step] = f32_pool.tile([P, CHUNK_COLS], F32, name="dist")
-                nc.scalar.activation(out=dist[step][:], in_=x_part, func=ACT.Abs, bias=minus_g, scale=1.0)
-            dist_sq[step] = f32_pool.tile([P, CHUNK_COLS], F32, name="dist_sq")
-            nc.scalar.activation(out=dist_sq[step][:], in_=x_part, func=ACT.Square, bias=minus_g, scale=1.0)
-            gap_sq[step] = f32_pool.tile([P, CHUNK_COLS], F32, name="gap_sq")
-            gap_bias = shift[:, g : g + 1] if is_end(step) else minus_one[:]
-            nc.scalar.activation(
-                out=gap_sq[step][:], in_=dist[step][:], func=ACT.Square, bias=gap_bias, scale=1.0
-            )
+            chunk, knots = knots_of(step)
+            dist_sq[step] = f32_pool.tile([P, STEP_COLS], F32, name="dist_sq")
+            for i, g in enumerate(knots):
+                nc.scalar.activation(
+                    out=dist_sq[step][:, i * KNOT_COLS : (i + 1) * KNOT_COLS],
+                    in_=x_grouped[chunk][:],
+                    func=ACT.Square,
+                    bias=minus_grid[:, g : g + 1],
+                    scale=1.0,
+                )
+
+        def gap_squares(step):
+            chunk, knots = knots_of(step)
+            gap_sq[step] = f32_pool.tile([P, STEP_COLS], F32, name="gap_sq", bufs=2)
+            for i, g in enumerate(knots):
+                for j in range(TILES):
+                    nc.scalar.activation(
+                        out=by_row(gap_sq[step][:, bank_cols(i, j)]),
+                        in_=rows_first(dist[step, i, j]),
+                        func=ACT.Square,
+                        bias=shift[:, g : g + 1],
+                        scale=1.0,
+                    )
+
+        def times_gap(step, out_tile, factor):
+            chunk, knots = knots_of(step)
+            for i, g in enumerate(knots):
+                for j in range(TILES):
+                    cols = bank_cols(i, j)
+                    nc.vector.scalar_tensor_tensor(
+                        out=by_row(out_tile[:, cols]),
+                        in0=rows_first(dist[step, i, j]),
+                        scalar=shift[:, g : g + 1],
+                        in1=by_row(factor[:, cols]),
+                        op0=ALU.add,
+                        op1=ALU.mult,
+                    )
 
         def inner_product(step):
-            nc.vector.scalar_tensor_tensor(
-                out=dist_sq[step][:],
-                in0=dist[step][:],
-                scalar=to_gap(step),
-                in1=dist_sq[step][:],
-                op0=ALU.add,
-                op1=ALU.mult,
-            )
+            times_gap(step, dist_sq[step], dist_sq[step])
 
         def inner_finish(step):
-            inner[step] = bf16_pool.tile([P, CHUNK_COLS], BF16, name="inner")
-            scalar_cols = SCALAR_COLS_AT_ENDS if is_end(step) else SCALAR_COLS
-            if step < GRID:
-                scalar_cols = 0
-            if scalar_cols > 0:
-                nc.scalar.activation(
-                    out=inner[step][:, :scalar_cols],
-                    in_=dist_sq[step][:, :scalar_cols],
-                    func=ACT.Identity,
-                    bias=minus_half[:],
-                    scale=-3.0,
-                )
-            nc.vector.tensor_scalar(
-                out=inner[step][:, scalar_cols:],
-                in0=dist_sq[step][:, scalar_cols:],
+            inner[step] = bf16_pool.tile([P, STEP_COLS], BF16, name="inner")
+            nc.gpsimd.tensor_scalar(
+                out=inner[step][:],
+                in0=dist_sq[step][:],
                 scalar1=-3.0,
                 scalar2=-0.5,
                 op0=ALU.mult,
@@ -259,28 +288,21 @@ def tile_advancedkanlayer_pa_kernel(
             )
 
         def outer_cubic(step):
-            outer[step] = bf16_pool.tile([P, CHUNK_COLS], BF16, name="outer")
-            nc.vector.scalar_tensor_tensor(
-                out=outer[step][:],
-                in0=dist[step][:],
-                scalar=to_gap(step),
-                in1=gap_sq[step][:],
-                op0=ALU.add,
-                op1=ALU.mult,
-            )
+            outer[step] = bf16_pool.tile([P, STEP_COLS], BF16, name="outer")
+            times_gap(step, outer[step], gap_sq[step])
 
         def pick(step):
             nc.vector.tensor_tensor(out=inner[step][:], in0=inner[step][:], in1=outer[step][:], op=ALU.max)
 
         def to_basis(step):
-            basis[step] = bf16_pool.tile([P, CHUNK_COLS], BF16, name="basis", align_bytes=64)
+            basis[step] = bf16_pool.tile([P, STEP_COLS], BF16, name="basis", align_bytes=64)
             nc.vector.tensor_scalar(
                 out=basis[step][:], in0=inner[step][:], scalar1=-2.0, scalar2=0.0, op0=ALU.mult, op1=ALU.max
             )
 
         def quantise_basis(step):
-            basis_codes[step] = code_pool.tile([P, CHUNK_ROWS], U32, name="basis_codes", align_bytes=64)
-            basis_scales[step] = code_pool.tile([P, CHUNK_ROWS], U8, name="basis_scales", align_bytes=64)
+            basis_codes[step] = code_pool.tile([P, KNOTS * ROWS], U32, name="basis_codes", align_bytes=64)
+            basis_scales[step] = code_pool.tile([P, KNOTS * ROWS], U8, name="basis_scales", align_bytes=64)
             nc.vector.quantize_mx(
                 out=basis_codes[step][:].bitcast(FP8X4), scales=basis_scales[step][:], in_=basis[step][:]
             )
@@ -288,65 +310,67 @@ def tile_advancedkanlayer_pa_kernel(
         spline_sum = {}
 
         def multiply(step):
-            chunk, g = divmod(step, GRID)
-            for j in range(TILES_PER_CHUNK):
-                if g == 0:
-                    spline_sum[j] = sum_banks.tile([P, OUTPUTS], F32, name="spline_sum")
-                rows = slice(j * P, (j + 1) * P)
-                nc.tensor.matmul_mx(
-                    out=spline_sum[j][:],
-                    lhsT=basis_codes[step][:, rows].bitcast(FP8X4),
-                    lhsT_scale=basis_scales[step][:, rows],
-                    rhs=weight_codes[:, g, :].bitcast(FP8X4),
-                    rhs_scale=weight_scales[:, g, :],
-                    start=(g == 0),
-                    stop=(g == GRID - 1),
-                )
+            chunk, knots = knots_of(step)
+            for i, g in enumerate(knots):
+                for j in range(TILES):
+                    if g == 0:
+                        spline_sum[j] = sum_banks.tile([P, OUTPUTS], F32, name="spline_sum")
+                    rows = slice((i * TILES + j) * P, (i * TILES + j + 1) * P)
+                    nc.tensor.matmul_mx(
+                        out=spline_sum[j][:],
+                        lhsT=basis_codes[step][:, rows].bitcast(FP8X4),
+                        lhsT_scale=basis_scales[step][:, rows],
+                        rhs=weight_codes[:, g, :].bitcast(FP8X4),
+                        rhs_scale=weight_scales[:, g, :],
+                        start=(g == 0),
+                        stop=(g == GRID - 1),
+                    )
 
         def finish(chunk):
-            for j in range(TILES_PER_CHUNK):
-                result = out_pool.tile([P, OUTPUTS], F32, name="result")
+            result = out_pool.tile([P, TILES, OUTPUTS], F32, name="result")
+            for j in range(TILES):
                 nc.vector.tensor_tensor(
-                    out=result[:], in0=spline_sum[j][:], in1=base_tenth[chunk][:, j, :], op=ALU.add
+                    out=result[:, j, :], in0=spline_sum[j][:], in1=base_tenth[chunk][:, j, :], op=ALU.add
                 )
-                nc.sync.dma_start(out=out_rows[:, chunk * TILES_PER_CHUNK + j, :], in_=result[:])
+            nc.sync.dma_start(out=out_rows[:, chunk * TILES : (chunk + 1) * TILES, :], in_=result[:])
 
         def is_step(step):
             return 0 <= step < STEPS
 
         turn_x(0)
-        end_distance(0)
-        for r in range(STEPS + 5):
-            chunk, g = divmod(r, GRID)
+        for r in range(-2, STEPS + 2):
+            chunk, pair = divmod(r, STEPS_PER_CHUNK)
             if is_step(r):
-                squares(r)
-            if r - 4 >= 0 and (r - 4) % GRID == GRID - 1:
-                finish((r - 4) // GRID)
+                inner_product(r)
+                inner_finish(r)
+            if pair == 1 and chunk >= 1:
+                finish(chunk - 1)
+            if is_step(r):
+                outer_cubic(r)
+            if is_step(r + 1):
+                turn_dist(r + 1)
+                gap_squares(r + 1)
+            if is_step(r + 2):
+                fold(r + 2)
+                squares(r + 2)
             if is_step(r - 1):
-                inner_product(r - 1)
-            if is_step(r - 2):
-                pick(r - 2)
+                to_basis(r - 1)
+            if is_step(r):
+                pick(r)
             if is_step(r - 1):
-                outer_cubic(r - 1)
-            if is_step(r - 2):
-                to_basis(r - 2)
+                quantise_basis(r - 1)
+            if 0 <= r < STEPS_PER_CHUNK:
+                for g in (KNOTS * r, KNOTS * r + 1):
+                    turn_weights(g)
+                for g in (KNOTS * r, KNOTS * r + 1):
+                    quantise_weights(g)
             if is_step(r - 1):
-                inner_finish(r - 1)
-            if is_step(r - 2):
-                quantise_basis(r - 2)
-            if 0 <= r - 2 < GRID:
-                quantise_weights(r - 2)
-            if is_step(r + 1) and is_end(r + 1):
-                end_distance(r + 1)
-            if 0 <= r - 1 < GRID:
-                turn_weights(r - 1)
-            if is_step(r - 3):
-                multiply(r - 3)
-            if is_step(r) and g == 1:
-                quantise_x(chunk)
-            if is_step(r) and g == 2:
-                base_product(chunk)
-            if g == GRID - 3 and chunk + 1 < CHUNKS:
+                multiply(r - 1)
+            if is_step(r) and pair == 0 and chunk + 1 < CHUNKS:
                 turn_x(chunk + 1)
                 if chunk + 2 < CHUNKS:
                     load_x(chunk + 2)
+            if is_step(r) and pair == 1:
+                quantise_x(chunk)
+            if is_step(r) and pair == 2:
+                base_product(chunk)

@@ -66,7 +66,7 @@ def tile_advancedkanlayer_pa_kernel(
         w4_scales = keep.tile([P, OUTPUTS], U8, align_bytes=64)
         grid_rows = keep.tile([P, GRID], BF16)
         minus_grid = keep.tile([P, GRID], F32)
-        shift = keep.tile([P, GRID], F32)
+        shift = keep.tile([P, GRID, P], F32)
         fold_bias = keep.tile([P, GRID], F32)
 
         nc.vector.memset(w4_scales[:].bitcast(I32), 0)
@@ -100,8 +100,8 @@ def tile_advancedkanlayer_pa_kernel(
         )
         for g, sign in ((LOW, -1.0), (HIGH, 1.0)):
             nc.vector.tensor_scalar(
-                out=shift[:, g : g + 1],
-                in0=grid_rows[:, g : g + 1],
+                out=shift[:, g, :],
+                in0=grid_rows[:, g : g + 1].to_broadcast([P, P]),
                 scalar1=sign,
                 scalar2=-1.0,
                 op0=ALU.mult,
@@ -115,7 +115,7 @@ def tile_advancedkanlayer_pa_kernel(
                 op0=ALU.mult,
             )
 
-        x_grouped, x_codes, x_scales, base_tenth = {}, {}, {}, {}
+        x_grouped, x_codes, x_scales, base_sum, base_tenth = {}, {}, {}, {}, {}
 
         def turn_x(chunk):
             turned = work_banks.tile([P, TILES, 2, P], F32, tag="bank")
@@ -137,12 +137,11 @@ def tile_advancedkanlayer_pa_kernel(
             )
 
         def base_product(chunk):
-            base_tenth[chunk] = out_pool.tile([P, TILES, OUTPUTS], F32, name="base_tenth")
             for j in range(TILES):
                 rows = slice(j * P, (j + 1) * P)
-                base_sum = work_banks.tile([P, OUTPUTS], F32, tag="bank")
+                base_sum[chunk, j] = work_banks.tile([P, OUTPUTS], F32, name="base_sum", tag="bank")
                 nc.tensor.matmul_mx(
-                    out=base_sum[:],
+                    out=base_sum[chunk, j][:],
                     lhsT=x_codes[chunk][:, rows].bitcast(FP8X4),
                     lhsT_scale=x_scales[chunk][:, rows],
                     rhs=w4_words[:].bitcast(FP4X4),
@@ -150,8 +149,16 @@ def tile_advancedkanlayer_pa_kernel(
                     start=True,
                     stop=True,
                 )
+
+        def base_finish(chunk):
+            base_tenth[chunk] = out_pool.tile([P, TILES, OUTPUTS], F32, name="base_tenth")
+            for j in range(TILES):
                 nc.vector.tensor_scalar(
-                    out=base_tenth[chunk][:, j, :], in0=base_sum[:], scalar1=0.1, scalar2=None, op0=ALU.mult
+                    out=base_tenth[chunk][:, j, :],
+                    in0=base_sum[chunk, j][:],
+                    scalar1=0.1,
+                    scalar2=None,
+                    op0=ALU.mult,
                 )
 
         weight_grouped = {}
@@ -220,9 +227,17 @@ def tile_advancedkanlayer_pa_kernel(
                             )
                         nc.tensor.matmul(
                             bank[:, t, :],
-                            lhsT=folded[step][:, i, j, t:FEATURES:PACK],
+                            lhsT=shift[:, g, :],
                             rhs=ident_f32[:],
                             start=g not in (LOW, HIGH),
+                            stop=False,
+                            is_transpose=True,
+                        )
+                        nc.tensor.matmul(
+                            bank[:, t, :],
+                            lhsT=folded[step][:, i, j, t:FEATURES:PACK],
+                            rhs=ident_f32[:],
+                            start=False,
                             stop=True,
                             is_transpose=True,
                         )
@@ -255,32 +270,30 @@ def tile_advancedkanlayer_pa_kernel(
                         out=by_row(gap_sq[step][:, bank_cols(i, j)]),
                         in_=rows_first(dist[step, i, j]),
                         func=ACT.Square,
-                        bias=shift[:, g : g + 1],
-                        scale=1.0,
                     )
 
-        def times_gap(step, out_tile, factor):
-            chunk, knots = knots_of(step)
-            for i, g in enumerate(knots):
-                for j in range(TILES):
-                    cols = bank_cols(i, j)
-                    nc.vector.scalar_tensor_tensor(
-                        out=by_row(out_tile[:, cols]),
-                        in0=rows_first(dist[step, i, j]),
-                        scalar=shift[:, g : g + 1],
-                        in1=by_row(factor[:, cols]),
-                        op0=ALU.add,
-                        op1=ALU.mult,
-                    )
+        def times_gap(step, i, out_tile, factor):
+            for j in range(TILES):
+                cols = bank_cols(i, j)
+                nc.vector.scalar_tensor_tensor(
+                    out=by_row(out_tile[:, cols]),
+                    in0=rows_first(dist[step, i, j]),
+                    scalar=0.0,
+                    in1=by_row(factor[:, cols]),
+                    op0=ALU.min,
+                    op1=ALU.mult,
+                )
 
-        def inner_product(step):
-            times_gap(step, dist_sq[step], dist_sq[step])
+        def inner_product(step, i):
+            times_gap(step, i, dist_sq[step], dist_sq[step])
 
-        def inner_finish(step):
-            inner[step] = bf16_pool.tile([P, STEP_COLS], BF16, name="inner")
+        def inner_finish(step, i):
+            if i == 0:
+                inner[step] = bf16_pool.tile([P, STEP_COLS], BF16, name="inner")
+            cols = slice(i * KNOT_COLS, (i + 1) * KNOT_COLS)
             nc.gpsimd.tensor_scalar(
-                out=inner[step][:],
-                in0=dist_sq[step][:],
+                out=inner[step][:, cols],
+                in0=dist_sq[step][:, cols],
                 scalar1=-3.0,
                 scalar2=-0.5,
                 op0=ALU.mult,
@@ -289,20 +302,16 @@ def tile_advancedkanlayer_pa_kernel(
 
         def outer_cubic(step):
             outer[step] = bf16_pool.tile([P, STEP_COLS], BF16, name="outer")
-            times_gap(step, outer[step], gap_sq[step])
+            for i in range(KNOTS):
+                times_gap(step, i, outer[step], gap_sq[step])
 
         def pick(step):
-            nc.vector.tensor_tensor(out=inner[step][:], in0=inner[step][:], in1=outer[step][:], op=ALU.max)
-
-        def to_basis(step):
             basis[step] = bf16_pool.tile([P, STEP_COLS], BF16, name="basis", align_bytes=64)
-            nc.vector.tensor_scalar(
-                out=basis[step][:], in0=inner[step][:], scalar1=-2.0, scalar2=0.0, op0=ALU.mult, op1=ALU.max
-            )
+            nc.vector.tensor_tensor(out=basis[step][:], in0=inner[step][:], in1=outer[step][:], op=ALU.max)
 
         def quantise_basis(step):
-            basis_codes[step] = code_pool.tile([P, KNOTS * ROWS], U32, name="basis_codes", align_bytes=64)
-            basis_scales[step] = code_pool.tile([P, KNOTS * ROWS], U8, name="basis_scales", align_bytes=64)
+            basis_codes[step] = code_pool.tile([P, KNOTS * ROWS], U32, name="basis_codes", align_bytes=64, bufs=7)
+            basis_scales[step] = code_pool.tile([P, KNOTS * ROWS], U8, name="basis_scales", align_bytes=64, bufs=7)
             nc.vector.quantize_mx(
                 out=basis_codes[step][:].bitcast(FP8X4), scales=basis_scales[step][:], in_=basis[step][:]
             )
@@ -329,8 +338,13 @@ def tile_advancedkanlayer_pa_kernel(
         def finish(chunk):
             result = out_pool.tile([P, TILES, OUTPUTS], F32, name="result")
             for j in range(TILES):
-                nc.vector.tensor_tensor(
-                    out=result[:, j, :], in0=spline_sum[j][:], in1=base_tenth[chunk][:, j, :], op=ALU.add
+                nc.vector.scalar_tensor_tensor(
+                    out=result[:, j, :],
+                    in0=spline_sum[j][:],
+                    scalar=-2.0,
+                    in1=base_tenth[chunk][:, j, :],
+                    op0=ALU.mult,
+                    op1=ALU.add,
                 )
             nc.sync.dma_start(out=out_rows[:, chunk * TILES : (chunk + 1) * TILES, :], in_=result[:])
 
@@ -338,39 +352,45 @@ def tile_advancedkanlayer_pa_kernel(
             return 0 <= step < STEPS
 
         turn_x(0)
+        finished = 0
+        next_step = 0
         for r in range(-2, STEPS + 2):
             chunk, pair = divmod(r, STEPS_PER_CHUNK)
             if is_step(r):
-                inner_product(r)
-                inner_finish(r)
-            if pair == 1 and chunk >= 1:
-                finish(chunk - 1)
+                for i in range(KNOTS):
+                    inner_product(r, i)
+                    inner_finish(r, i)
+            if is_step(r) and pair == 3:
+                base_finish(chunk)
+            if next_step > 0 and next_step % STEPS_PER_CHUNK == 0 and next_step // STEPS_PER_CHUNK > finished:
+                finish(finished)
+                finished += 1
             if is_step(r):
                 outer_cubic(r)
             if is_step(r + 1):
                 turn_dist(r + 1)
                 gap_squares(r + 1)
-            if is_step(r + 2):
-                fold(r + 2)
-                squares(r + 2)
-            if is_step(r - 1):
-                to_basis(r - 1)
-            if is_step(r):
-                pick(r)
-            if is_step(r - 1):
-                quantise_basis(r - 1)
-            if 0 <= r < STEPS_PER_CHUNK:
-                for g in (KNOTS * r, KNOTS * r + 1):
-                    turn_weights(g)
-                for g in (KNOTS * r, KNOTS * r + 1):
-                    quantise_weights(g)
-            if is_step(r - 1):
-                multiply(r - 1)
+            if 0 <= r < GRID:
+                turn_weights(r)
             if is_step(r) and pair == 0 and chunk + 1 < CHUNKS:
                 turn_x(chunk + 1)
                 if chunk + 2 < CHUNKS:
                     load_x(chunk + 2)
-            if is_step(r) and pair == 1:
-                quantise_x(chunk)
             if is_step(r) and pair == 2:
                 base_product(chunk)
+            if is_step(r + 2):
+                fold(r + 2)
+                squares(r + 2)
+            if is_step(r - 1):
+                quantise_basis(r - 1)
+            if is_step(r):
+                pick(r)
+            if 0 <= r - 1 < GRID:
+                quantise_weights(r - 1)
+            for turn in range(2):
+                last_knot = next_step % STEPS_PER_CHUNK * KNOTS + KNOTS - 1
+                if next_step <= r - 1 and next_step < STEPS and last_knot + 1 <= r and next_step // STEPS_PER_CHUNK == finished:
+                    multiply(next_step)
+                    next_step += 1
+            if is_step(r) and pair == 1:
+                quantise_x(chunk)

@@ -117,6 +117,15 @@ def tile_advancedkanlayer_pa_kernel(
 
         x_grouped, x_codes, x_scales, base_sum, base_tenth = {}, {}, {}, {}, {}
 
+        x_split = {}
+
+        def split_x(chunk):
+            x_split[chunk] = x_pool.tile([P, TILES, FEATURES], BF16, name="x_split")
+            nc.vector.tensor_copy(
+                out=x_split[chunk][:].rearrange("p j (t q) -> p j t q", t=PACK),
+                in_=x_raw[chunk][:].rearrange("p j (q t) -> p j t q", t=PACK),
+            )
+
         def turn_x(chunk):
             turned = work_banks.tile([P, TILES, 2, P], F32, tag="bank")
             for j in range(TILES):
@@ -208,7 +217,7 @@ def tile_advancedkanlayer_pa_kernel(
                 else:
                     func, bias, scale = ACT.Abs, minus_grid[:, g : g + 1], 1.0
                 nc.scalar.activation(
-                    out=folded[step][:, i, :, :], in_=x_raw[chunk][:], func=func, bias=bias, scale=scale
+                    out=folded[step][:, i, :, :], in_=x_split[chunk][:], func=func, bias=bias, scale=scale
                 )
 
         def turn_dist(step):
@@ -220,7 +229,7 @@ def tile_advancedkanlayer_pa_kernel(
                         if g in (LOW, HIGH):
                             nc.tensor.matmul(
                                 bank[:, t, :],
-                                lhsT=x_raw[chunk][:, j, t:FEATURES:PACK],
+                                lhsT=x_split[chunk][:, j, t * P : (t + 1) * P],
                                 rhs=ident_bf16[:] if g == LOW else minus_ident[:],
                                 start=True,
                                 stop=False,
@@ -235,7 +244,7 @@ def tile_advancedkanlayer_pa_kernel(
                         )
                         nc.tensor.matmul(
                             bank[:, t, :],
-                            lhsT=folded[step][:, i, j, t:FEATURES:PACK],
+                            lhsT=folded[step][:, i, j, t * P : (t + 1) * P],
                             rhs=ident_f32[:],
                             start=False,
                             stop=True,
@@ -351,6 +360,7 @@ def tile_advancedkanlayer_pa_kernel(
         def is_step(step):
             return 0 <= step < STEPS
 
+        split_x(0)
         turn_x(0)
         finished = 0
         next_step = 0
@@ -392,5 +402,7 @@ def tile_advancedkanlayer_pa_kernel(
                 if next_step <= r - 1 and next_step < STEPS and last_knot + 1 <= r and next_step // STEPS_PER_CHUNK == finished:
                     multiply(next_step)
                     next_step += 1
+            if is_step(r) and pair == 0 and chunk + 1 < CHUNKS:
+                split_x(chunk + 1)
             if is_step(r) and pair == 1:
                 quantise_x(chunk)

@@ -66,7 +66,7 @@ def tile_advancedkanlayer_pa_kernel(
         w4_scales = keep.tile([P, OUTPUTS], U8, align_bytes=64)
         grid_rows = keep.tile([P, GRID], BF16)
         minus_grid = keep.tile([P, GRID], F32)
-        shift = keep.tile([P, GRID, P], F32)
+        shift = keep.tile([P, GRID], F32)
         fold_bias = keep.tile([P, GRID], F32)
 
         nc.vector.memset(w4_scales[:].bitcast(I32), 0)
@@ -100,8 +100,8 @@ def tile_advancedkanlayer_pa_kernel(
         )
         for g, sign in ((LOW, -1.0), (HIGH, 1.0)):
             nc.vector.tensor_scalar(
-                out=shift[:, g, :],
-                in0=grid_rows[:, g : g + 1].to_broadcast([P, P]),
+                out=shift[:, g : g + 1],
+                in0=grid_rows[:, g : g + 1],
                 scalar1=sign,
                 scalar2=-1.0,
                 op0=ALU.mult,
@@ -202,55 +202,50 @@ def tile_advancedkanlayer_pa_kernel(
             chunk, pair = divmod(step, STEPS_PER_CHUNK)
             return chunk, [pair * KNOTS + i for i in range(KNOTS)]
 
-        def bank_cols(i, j):
-            first = i * KNOT_COLS + j * BANK
-            return slice(first, first + BANK)
+        def is_step(step):
+            return 0 <= step < STEPS
 
-        def fold(step):
+        def bank_cols(b):
+            return slice(b * BANK, (b + 1) * BANK)
+
+        def fold(step, i):
             chunk, knots = knots_of(step)
-            folded[step] = f32_pool.tile([P, KNOTS, TILES, FEATURES], F32, name="folded", bufs=2)
-            for i, g in enumerate(knots):
-                if g == LOW:
-                    func, bias, scale = ACT.Relu, fold_bias[:, g : g + 1], -2.0
-                elif g == HIGH:
-                    func, bias, scale = ACT.Relu, fold_bias[:, g : g + 1], 2.0
-                else:
-                    func, bias, scale = ACT.Abs, minus_grid[:, g : g + 1], 1.0
-                nc.scalar.activation(
-                    out=folded[step][:, i, :, :], in_=x_split[chunk][:], func=func, bias=bias, scale=scale
+            g = knots[i]
+            if i == 0:
+                folded[step] = f32_pool.tile([P, KNOTS, TILES, FEATURES], F32, name="folded", bufs=2)
+            if g == LOW:
+                func, bias, scale = ACT.Relu, fold_bias[:, g : g + 1], -2.0
+            elif g == HIGH:
+                func, bias, scale = ACT.Relu, fold_bias[:, g : g + 1], 2.0
+            else:
+                func, bias, scale = ACT.Abs, minus_grid[:, g : g + 1], 1.0
+            nc.scalar.activation(
+                out=folded[step][:, i, :, :], in_=x_split[chunk][:], func=func, bias=bias, scale=scale
+            )
+
+        def turn_dist(step, b):
+            chunk, knots = knots_of(step)
+            i, j = divmod(b, TILES)
+            g = knots[i]
+            bank = dist_banks.tile([P, PACK, P], F32, name="dist")
+            for t in range(PACK):
+                if g in (LOW, HIGH):
+                    nc.tensor.matmul(
+                        bank[:, t, :],
+                        lhsT=x_split[chunk][:, j, t * P : (t + 1) * P],
+                        rhs=ident_bf16[:] if g == LOW else minus_ident[:],
+                        start=True,
+                        stop=False,
+                    )
+                nc.tensor.matmul(
+                    bank[:, t, :],
+                    lhsT=folded[step][:, i, j, t * P : (t + 1) * P],
+                    rhs=ident_f32[:],
+                    start=g not in (LOW, HIGH),
+                    stop=True,
+                    is_transpose=True,
                 )
-
-        def turn_dist(step):
-            chunk, knots = knots_of(step)
-            for i, g in enumerate(knots):
-                for j in range(TILES):
-                    bank = dist_banks.tile([P, PACK, P], F32, name="dist")
-                    for t in range(PACK):
-                        if g in (LOW, HIGH):
-                            nc.tensor.matmul(
-                                bank[:, t, :],
-                                lhsT=x_split[chunk][:, j, t * P : (t + 1) * P],
-                                rhs=ident_bf16[:] if g == LOW else minus_ident[:],
-                                start=True,
-                                stop=False,
-                            )
-                        nc.tensor.matmul(
-                            bank[:, t, :],
-                            lhsT=shift[:, g, :],
-                            rhs=ident_f32[:],
-                            start=g not in (LOW, HIGH),
-                            stop=False,
-                            is_transpose=True,
-                        )
-                        nc.tensor.matmul(
-                            bank[:, t, :],
-                            lhsT=folded[step][:, i, j, t * P : (t + 1) * P],
-                            rhs=ident_f32[:],
-                            start=False,
-                            stop=True,
-                            is_transpose=True,
-                        )
-                    dist[step, i, j] = bank
+            dist[step, b] = bank
 
         def rows_first(bank):
             return bank[:].rearrange("p t r -> p r t")
@@ -258,47 +253,48 @@ def tile_advancedkanlayer_pa_kernel(
         def by_row(tile_cols):
             return tile_cols.rearrange("p (r t) -> p r t", t=PACK)
 
-        def squares(step):
+        def square(step, i):
             chunk, knots = knots_of(step)
-            dist_sq[step] = f32_pool.tile([P, STEP_COLS], F32, name="dist_sq")
-            for i, g in enumerate(knots):
-                nc.scalar.activation(
-                    out=dist_sq[step][:, i * KNOT_COLS : (i + 1) * KNOT_COLS],
-                    in_=x_grouped[chunk][:],
-                    func=ACT.Square,
-                    bias=minus_grid[:, g : g + 1],
-                    scale=1.0,
-                )
+            if i == 0:
+                dist_sq[step] = f32_pool.tile([P, STEP_COLS], F32, name="dist_sq")
+            nc.scalar.activation(
+                out=dist_sq[step][:, i * KNOT_COLS : (i + 1) * KNOT_COLS],
+                in_=x_grouped[chunk][:],
+                func=ACT.Square,
+                bias=minus_grid[:, knots[i] : knots[i] + 1],
+                scale=1.0,
+            )
 
-        def gap_squares(step):
-            chunk, knots = knots_of(step)
-            gap_sq[step] = f32_pool.tile([P, STEP_COLS], F32, name="gap_sq", bufs=2)
-            for i, g in enumerate(knots):
-                for j in range(TILES):
-                    nc.scalar.activation(
-                        out=by_row(gap_sq[step][:, bank_cols(i, j)]),
-                        in_=rows_first(dist[step, i, j]),
-                        func=ACT.Square,
-                    )
+        def gap_square(step, b):
+            g = knots_of(step)[1][b // TILES]
+            if b == 0:
+                gap_sq[step] = f32_pool.tile([P, STEP_COLS], F32, name="gap_sq", bufs=2)
+            nc.scalar.activation(
+                out=by_row(gap_sq[step][:, bank_cols(b)]),
+                in_=rows_first(dist[step, b]),
+                func=ACT.Square,
+                bias=shift[:, g : g + 1],
+                scale=1.0,
+            )
 
-        def times_gap(step, i, out_tile, factor):
-            for j in range(TILES):
-                cols = bank_cols(i, j)
-                nc.vector.scalar_tensor_tensor(
-                    out=by_row(out_tile[:, cols]),
-                    in0=rows_first(dist[step, i, j]),
-                    scalar=0.0,
-                    in1=by_row(factor[:, cols]),
-                    op0=ALU.min,
-                    op1=ALU.mult,
-                )
+        def times_gap(step, b, out_tile, factor):
+            g = knots_of(step)[1][b // TILES]
+            cols = bank_cols(b)
+            nc.vector.scalar_tensor_tensor(
+                out=by_row(out_tile[:, cols]),
+                in0=rows_first(dist[step, b]),
+                scalar=shift[:, g : g + 1],
+                in1=by_row(factor[:, cols]),
+                op0=ALU.add,
+                op1=ALU.mult,
+            )
 
-        def inner_product(step, i):
-            times_gap(step, i, dist_sq[step], dist_sq[step])
+        def inner_product(step, b):
+            times_gap(step, b, dist_sq[step], dist_sq[step])
 
         def inner_finish(step, i):
             if i == 0:
-                inner[step] = bf16_pool.tile([P, STEP_COLS], BF16, name="inner")
+                inner[step] = bf16_pool.tile([P, STEP_COLS], BF16, name="inner", bufs=3)
             cols = slice(i * KNOT_COLS, (i + 1) * KNOT_COLS)
             nc.gpsimd.tensor_scalar(
                 out=inner[step][:, cols],
@@ -309,14 +305,19 @@ def tile_advancedkanlayer_pa_kernel(
                 op1=ALU.add,
             )
 
-        def outer_cubic(step):
-            outer[step] = bf16_pool.tile([P, STEP_COLS], BF16, name="outer")
-            for i in range(KNOTS):
-                times_gap(step, i, outer[step], gap_sq[step])
+        def outer_cubic(step, b):
+            if b == 0:
+                outer[step] = bf16_pool.tile([P, STEP_COLS], BF16, name="outer", bufs=3)
+            times_gap(step, b, outer[step], gap_sq[step])
 
         def pick(step):
+            nc.vector.tensor_tensor(out=inner[step][:], in0=inner[step][:], in1=outer[step][:], op=ALU.max)
+
+        def to_basis(step):
             basis[step] = bf16_pool.tile([P, STEP_COLS], BF16, name="basis", align_bytes=64)
-            nc.vector.tensor_tensor(out=basis[step][:], in0=inner[step][:], in1=outer[step][:], op=ALU.max)
+            nc.vector.tensor_scalar(
+                out=basis[step][:], in0=inner[step][:], scalar1=0.0, scalar2=None, op0=ALU.min
+            )
 
         def quantise_basis(step):
             basis_codes[step] = code_pool.tile([P, KNOTS * ROWS], U32, name="basis_codes", align_bytes=64, bufs=7)
@@ -357,29 +358,53 @@ def tile_advancedkanlayer_pa_kernel(
                 )
             nc.sync.dma_start(out=out_rows[:, chunk * TILES : (chunk + 1) * TILES, :], in_=result[:])
 
-        def is_step(step):
-            return 0 <= step < STEPS
-
         split_x(0)
         turn_x(0)
         finished = 0
         next_step = 0
-        for r in range(-2, STEPS + 2):
+        for r in range(-2, STEPS + 3):
             chunk, pair = divmod(r, STEPS_PER_CHUNK)
-            if is_step(r):
-                for i in range(KNOTS):
-                    inner_product(r, i)
-                    inner_finish(r, i)
+            for b in range(BANKS):
+                if is_step(r):
+                    inner_product(r, b)
+                    if b % TILES == TILES - 1:
+                        inner_finish(r, b // TILES)
+                    outer_cubic(r, b)
+                if is_step(r + 1):
+                    turn_dist(r + 1, b)
+                    gap_square(r + 1, b)
+                if is_step(r + 2):
+                    (fold, fold, square, square)[b](r + 2, b % KNOTS)
+                if b == 0:
+                    if is_step(r - 1):
+                        pick(r - 1)
+                    if is_step(r - 2):
+                        quantise_basis(r - 2)
+                    if 0 <= r - 2 < GRID:
+                        quantise_weights(r - 2)
+                    if is_step(r) and pair == 1:
+                        quantise_x(chunk)
+                    if next_step == (finished + 1) * STEPS_PER_CHUNK:
+                        finish(finished)
+                        finished += 1
+                if b == 1:
+                    for turn in range(2):
+                        last_knot = next_step % STEPS_PER_CHUNK * KNOTS + KNOTS - 1
+                        if (
+                            next_step <= r - 2
+                            and next_step < STEPS
+                            and last_knot + 2 <= r
+                            and next_step // STEPS_PER_CHUNK == finished
+                        ):
+                            multiply(next_step)
+                            next_step += 1
+                if b == 2:
+                    if is_step(r - 1):
+                        to_basis(r - 1)
+                    if is_step(r) and pair == 0 and chunk + 1 < CHUNKS:
+                        split_x(chunk + 1)
             if is_step(r) and pair == 3:
                 base_finish(chunk)
-            if next_step > 0 and next_step % STEPS_PER_CHUNK == 0 and next_step // STEPS_PER_CHUNK > finished:
-                finish(finished)
-                finished += 1
-            if is_step(r):
-                outer_cubic(r)
-            if is_step(r + 1):
-                turn_dist(r + 1)
-                gap_squares(r + 1)
             if 0 <= r < GRID:
                 turn_weights(r)
             if is_step(r) and pair == 0 and chunk + 1 < CHUNKS:
@@ -388,21 +413,3 @@ def tile_advancedkanlayer_pa_kernel(
                     load_x(chunk + 2)
             if is_step(r) and pair == 2:
                 base_product(chunk)
-            if is_step(r + 2):
-                fold(r + 2)
-                squares(r + 2)
-            if is_step(r - 1):
-                quantise_basis(r - 1)
-            if is_step(r):
-                pick(r)
-            if 0 <= r - 1 < GRID:
-                quantise_weights(r - 1)
-            for turn in range(2):
-                last_knot = next_step % STEPS_PER_CHUNK * KNOTS + KNOTS - 1
-                if next_step <= r - 1 and next_step < STEPS and last_knot + 1 <= r and next_step // STEPS_PER_CHUNK == finished:
-                    multiply(next_step)
-                    next_step += 1
-            if is_step(r) and pair == 0 and chunk + 1 < CHUNKS:
-                split_x(chunk + 1)
-            if is_step(r) and pair == 1:
-                quantise_x(chunk)

@@ -160,15 +160,9 @@ def tile_advancedkanlayer_pa_kernel(
                 )
 
         def base_finish(chunk):
-            base_tenth[chunk] = out_pool.tile([P, TILES, OUTPUTS], F32, name="base_tenth")
+            base_tenth[chunk] = out_pool.tile([P, TILES, OUTPUTS], F32, name="base_tenth", bufs=3)
             for j in range(TILES):
-                nc.vector.tensor_scalar(
-                    out=base_tenth[chunk][:, j, :],
-                    in0=base_sum[chunk, j][:],
-                    scalar1=0.1,
-                    scalar2=None,
-                    op0=ALU.mult,
-                )
+                nc.scalar.mul(out=base_tenth[chunk][:, j, :], in_=base_sum[chunk, j][:], mul=0.1)
 
         weight_grouped = {}
 
@@ -359,10 +353,20 @@ def tile_advancedkanlayer_pa_kernel(
             nc.sync.dma_start(out=out_rows[:, chunk * TILES : (chunk + 1) * TILES, :], in_=result[:])
 
         split_x(0)
+        fold(0, 0)
         turn_x(0)
+        for i in range(KNOTS):
+            if i > 0:
+                fold(0, i)
+            square(0, i)
+            for j in range(TILES):
+                turn_dist(0, i * TILES + j)
+                gap_square(0, i * TILES + j)
+        for n in range(BANKS):
+            (fold, fold, square, square)[n](1, n % KNOTS)
         finished = 0
         next_step = 0
-        for r in range(-2, STEPS + 3):
+        for r in range(STEPS + 3):
             chunk, pair = divmod(r, STEPS_PER_CHUNK)
             for b in range(BANKS):
                 if is_step(r):
@@ -403,13 +407,13 @@ def tile_advancedkanlayer_pa_kernel(
                         to_basis(r - 1)
                     if is_step(r) and pair == 0 and chunk + 1 < CHUNKS:
                         split_x(chunk + 1)
-            if is_step(r) and pair == 3:
-                base_finish(chunk)
-            if 0 <= r < GRID:
+            if r < GRID:
                 turn_weights(r)
             if is_step(r) and pair == 0 and chunk + 1 < CHUNKS:
                 turn_x(chunk + 1)
                 if chunk + 2 < CHUNKS:
                     load_x(chunk + 2)
-            if is_step(r) and pair == 2:
-                base_product(chunk)
+            for c in range(CHUNKS):
+                if r == max(c * STEPS_PER_CHUNK + 2, GRID + c):
+                    base_product(c)
+                    base_finish(c)

@@ -286,13 +286,12 @@ def tile_advancedkanlayer_pa_kernel(
         def inner_product(step, b):
             times_gap(step, b, dist_sq[step], dist_sq[step])
 
-        def inner_finish(step, i):
-            if i == 0:
+        def inner_finish(step, b):
+            if b == 0:
                 inner[step] = bf16_pool.tile([P, STEP_COLS], BF16, name="inner", bufs=3)
-            cols = slice(i * KNOT_COLS, (i + 1) * KNOT_COLS)
             nc.gpsimd.tensor_scalar(
-                out=inner[step][:, cols],
-                in0=dist_sq[step][:, cols],
+                out=inner[step][:, bank_cols(b)],
+                in0=dist_sq[step][:, bank_cols(b)],
                 scalar1=-3.0,
                 scalar2=-0.5,
                 op0=ALU.mult,
@@ -366,47 +365,45 @@ def tile_advancedkanlayer_pa_kernel(
             (fold, fold, square, square)[n](1, n % KNOTS)
         finished = 0
         next_step = 0
-        for r in range(STEPS + 3):
+        for r in range(STEPS + 2):
             chunk, pair = divmod(r, STEPS_PER_CHUNK)
-            for b in range(BANKS):
-                if is_step(r):
+            for product, b in ((0, 0), (1, 0), (0, 1), (1, 1), (0, 2), (0, 3), (1, 2), (1, 3)):
+                if product == 0 and is_step(r):
                     inner_product(r, b)
-                    if b % TILES == TILES - 1:
-                        inner_finish(r, b // TILES)
-                    outer_cubic(r, b)
-                if is_step(r + 1):
-                    turn_dist(r + 1, b)
-                    gap_square(r + 1, b)
-                if is_step(r + 2):
-                    (fold, fold, square, square)[b](r + 2, b % KNOTS)
-                if b == 0:
-                    if is_step(r - 1):
-                        pick(r - 1)
-                    if is_step(r - 2):
-                        quantise_basis(r - 2)
-                    if 0 <= r - 2 < GRID:
-                        quantise_weights(r - 2)
-                    if is_step(r) and pair == 1:
-                        quantise_x(chunk)
-                    if next_step == (finished + 1) * STEPS_PER_CHUNK:
-                        finish(finished)
-                        finished += 1
-                if b == 1:
-                    for turn in range(2):
-                        last_knot = next_step % STEPS_PER_CHUNK * KNOTS + KNOTS - 1
-                        if (
-                            next_step <= r - 2
-                            and next_step < STEPS
-                            and last_knot + 2 <= r
-                            and next_step // STEPS_PER_CHUNK == finished
-                        ):
-                            multiply(next_step)
-                            next_step += 1
-                if b == 2:
-                    if is_step(r - 1):
-                        to_basis(r - 1)
-                    if is_step(r) and pair == 0 and chunk + 1 < CHUNKS:
-                        split_x(chunk + 1)
+                    inner_finish(r, b)
+                if product == 1:
+                    if is_step(r):
+                        outer_cubic(r, b)
+                    if is_step(r + 1):
+                        turn_dist(r + 1, b)
+                        gap_square(r + 1, b)
+                    if is_step(r + 2):
+                        (fold, fold, square, square)[b](r + 2, b % KNOTS)
+            if next_step == (finished + 1) * STEPS_PER_CHUNK:
+                finish(finished)
+                finished += 1
+            if is_step(r - 1):
+                to_basis(r - 1)
+            if is_step(r):
+                pick(r)
+            if is_step(r - 1):
+                quantise_basis(r - 1)
+            if 0 <= r - 2 < GRID:
+                quantise_weights(r - 2)
+            if is_step(r) and pair == 1:
+                quantise_x(chunk)
+            if is_step(r) and pair == 0 and chunk + 1 < CHUNKS:
+                split_x(chunk + 1)
+            for turn in range(2):
+                last_knot = next_step % STEPS_PER_CHUNK * KNOTS + KNOTS - 1
+                if (
+                    next_step <= (r - 2 if r < STEPS else r - 1)
+                    and next_step < STEPS
+                    and last_knot + 2 <= r
+                    and next_step // STEPS_PER_CHUNK == finished
+                ):
+                    multiply(next_step)
+                    next_step += 1
             if r < GRID:
                 turn_weights(r)
             if is_step(r) and pair == 0 and chunk + 1 < CHUNKS:
@@ -414,6 +411,6 @@ def tile_advancedkanlayer_pa_kernel(
                 if chunk + 2 < CHUNKS:
                     load_x(chunk + 2)
             for c in range(CHUNKS):
-                if r == max(c * STEPS_PER_CHUNK + 2, GRID + c):
+                if r == max(c * STEPS_PER_CHUNK + 2, GRID + 1 + c):
                     base_product(c)
                     base_finish(c)

@@ -27,6 +27,9 @@ BANK = P * PACK
 KNOT_COLS = TILES * BANK
 STEP_COLS = KNOTS * KNOT_COLS
 BANKS = KNOTS * TILES
+ALL_COLS = slice(0, STEP_COLS)
+KNOT_SLICES = [slice(i * KNOT_COLS, (i + 1) * KNOT_COLS) for i in range(KNOTS)]
+LAST = STEPS - 1
 OUT_BLOCKS = OUTPUTS // P
 
 FLOPS = 2 * BATCH * OUTPUTS * (FEATURES * GRID + FEATURES)
@@ -166,21 +169,25 @@ def tile_advancedkanlayer_pa_kernel(
 
         weight_grouped = {}
 
-        def turn_weights(g):
-            weight_grouped[g] = bf16_pool.tile([P, OUTPUTS, PACK], BF16, name="weight_grouped", align_bytes=64)
-            for half in range(2):
-                turned = work_banks.tile([P, PACK, 2 * P], BF16, tag="bank")
+        def turn_weights(pair, half):
+            if half == 0:
+                for e in range(2):
+                    weight_grouped[2 * pair + e] = bf16_pool.tile(
+                        [P, OUTPUTS, PACK], BF16, name="weight_grouped", align_bytes=64, bufs=4
+                    )
+            for m in range(2 * half, 2 * half + 2):
+                words = weight_raw[:, m, :].bitcast(F32)
+                turned = work_banks.tile([P, PACK, P], F32, tag="bank")
                 for t in range(PACK):
-                    for j in range(2):
-                        nc.tensor.transpose(
-                            turned[:, t, j * P : (j + 1) * P],
-                            weight_raw[:, 2 * half + j, 8 * t + g : FEATURES * GRID : 8 * PACK],
-                            ident_bf16[:],
-                        )
-                nc.scalar.copy(
-                    out=weight_grouped[g][:, half * 2 * P : (half + 1) * 2 * P, :],
-                    in_=turned[:].rearrange("p t o -> p o t"),
-                )
+                    nc.tensor.transpose(
+                        turned[:, t, :], words[:, 4 * t + pair : FEATURES * GRID // 2 : 4 * PACK], ident_f32[:]
+                    )
+                values = turned[:].rearrange("p t o -> p (t o)").bitcast(BF16)
+                values = values.rearrange("p (t o e) -> p e o t", t=PACK, e=2)
+                for e in range(2):
+                    nc.scalar.copy(
+                        out=weight_grouped[2 * pair + e][:, m * P : (m + 1) * P, :], in_=values[:, e, :, :]
+                    )
 
         def quantise_weights(g):
             nc.vector.quantize_mx(
@@ -199,14 +206,27 @@ def tile_advancedkanlayer_pa_kernel(
         def is_step(step):
             return 0 <= step < STEPS
 
+        def on_vector(step, i):
+            return step < GRID + 2 and knots_of(step)[1][i] in (LOW, HIGH)
+
         def bank_cols(b):
             return slice(b * BANK, (b + 1) * BANK)
 
         def fold(step, i):
             chunk, knots = knots_of(step)
             g = knots[i]
-            if i == 0:
+            if step not in folded:
                 folded[step] = f32_pool.tile([P, KNOTS, TILES, FEATURES], F32, name="folded", bufs=2)
+            if on_vector(step, i):
+                nc.vector.tensor_scalar(
+                    out=folded[step][:, i, :, :],
+                    in0=x_split[chunk][:],
+                    scalar1=2.0 if g == LOW else -2.0,
+                    scalar2=fold_bias[:, g : g + 1],
+                    op0=ALU.mult,
+                    op1=ALU.max,
+                )
+                return
             if g == LOW:
                 func, bias, scale = ACT.Relu, fold_bias[:, g : g + 1], -2.0
             elif g == HIGH:
@@ -227,7 +247,7 @@ def tile_advancedkanlayer_pa_kernel(
                     nc.tensor.matmul(
                         bank[:, t, :],
                         lhsT=x_split[chunk][:, j, t * P : (t + 1) * P],
-                        rhs=ident_bf16[:] if g == LOW else minus_ident[:],
+                        rhs=ident_bf16[:] if (g == LOW) != on_vector(step, i) else minus_ident[:],
                         start=True,
                         stop=False,
                     )
@@ -303,27 +323,39 @@ def tile_advancedkanlayer_pa_kernel(
                 outer[step] = bf16_pool.tile([P, STEP_COLS], BF16, name="outer", bufs=3)
             times_gap(step, b, outer[step], gap_sq[step])
 
-        def pick(step):
-            nc.vector.tensor_tensor(out=inner[step][:], in0=inner[step][:], in1=outer[step][:], op=ALU.max)
-
-        def to_basis(step):
-            basis[step] = bf16_pool.tile([P, STEP_COLS], BF16, name="basis", align_bytes=64)
-            nc.vector.tensor_scalar(
-                out=basis[step][:], in0=inner[step][:], scalar1=0.0, scalar2=None, op0=ALU.min
+        def pick(step, cols=ALL_COLS):
+            nc.vector.tensor_tensor(
+                out=inner[step][:, cols], in0=inner[step][:, cols], in1=outer[step][:, cols], op=ALU.max
             )
 
-        def quantise_basis(step):
-            basis_codes[step] = code_pool.tile([P, KNOTS * ROWS], U32, name="basis_codes", align_bytes=64, bufs=7)
-            basis_scales[step] = code_pool.tile([P, KNOTS * ROWS], U8, name="basis_scales", align_bytes=64, bufs=7)
+        def to_basis(step, cols=ALL_COLS):
+            if cols.start == 0:
+                basis[step] = bf16_pool.tile([P, STEP_COLS], BF16, name="basis", align_bytes=64)
+            nc.vector.tensor_scalar(
+                out=basis[step][:, cols], in0=inner[step][:, cols], scalar1=0.0, scalar2=None, op0=ALU.min
+            )
+
+        def quantise_basis(step, cols=ALL_COLS):
+            if cols.start == 0:
+                basis_codes[step] = code_pool.tile(
+                    [P, KNOTS * ROWS], U32, name="basis_codes", align_bytes=64, bufs=7
+                )
+                basis_scales[step] = code_pool.tile(
+                    [P, KNOTS * ROWS], U8, name="basis_scales", align_bytes=64, bufs=7
+                )
+            words = slice(cols.start // PACK, cols.stop // PACK)
             nc.vector.quantize_mx(
-                out=basis_codes[step][:].bitcast(FP8X4), scales=basis_scales[step][:], in_=basis[step][:]
+                out=basis_codes[step][:, words].bitcast(FP8X4),
+                scales=basis_scales[step][:, words],
+                in_=basis[step][:, cols],
             )
 
         spline_sum = {}
 
-        def multiply(step):
+        def multiply(step, which=range(KNOTS)):
             chunk, knots = knots_of(step)
-            for i, g in enumerate(knots):
+            for i in which:
+                g = knots[i]
                 for j in range(TILES):
                     if g == 0:
                         spline_sum[j] = sum_banks.tile([P, OUTPUTS], F32, name="spline_sum")
@@ -349,7 +381,18 @@ def tile_advancedkanlayer_pa_kernel(
                     op0=ALU.mult,
                     op1=ALU.add,
                 )
-            nc.sync.dma_start(out=out_rows[:, chunk * TILES : (chunk + 1) * TILES, :], in_=result[:])
+                nc.sync.dma_start(out=out_rows[:, chunk * TILES + j, :], in_=result[:, j, :])
+
+        def scalar_part(step, n):
+            if n >= KNOTS:
+                square(step, n - KNOTS)
+            elif not on_vector(step, n):
+                fold(step, n)
+
+        def vector_folds(step):
+            for i in range(KNOTS):
+                if on_vector(step, i):
+                    fold(step, i)
 
         split_x(0)
         fold(0, 0)
@@ -362,51 +405,71 @@ def tile_advancedkanlayer_pa_kernel(
                 turn_dist(0, i * TILES + j)
                 gap_square(0, i * TILES + j)
         for n in range(BANKS):
-            (fold, fold, square, square)[n](1, n % KNOTS)
+            scalar_part(1, n)
+        vector_folds(1)
         finished = 0
         next_step = 0
-        for r in range(STEPS + 2):
+        for r in range(STEPS):
             chunk, pair = divmod(r, STEPS_PER_CHUNK)
             for product, b in ((0, 0), (1, 0), (0, 1), (1, 1), (0, 2), (0, 3), (1, 2), (1, 3)):
-                if product == 0 and is_step(r):
+                if product == 0:
                     inner_product(r, b)
                     inner_finish(r, b)
                 if product == 1:
-                    if is_step(r):
-                        outer_cubic(r, b)
+                    outer_cubic(r, b)
                     if is_step(r + 1):
                         turn_dist(r + 1, b)
                         gap_square(r + 1, b)
                     if is_step(r + 2):
-                        (fold, fold, square, square)[b](r + 2, b % KNOTS)
+                        scalar_part(r + 2, b)
+                if r == LAST and (product, b) == (0, 0):
+                    to_basis(r - 1)
+                if r == LAST and (product, b) == (0, 1):
+                    quantise_basis(r - 1)
+                if r == LAST and (product, b) == (0, 3):
+                    pick(r, KNOT_SLICES[0])
+                if r == LAST and (product, b) == (1, 2):
+                    to_basis(r, KNOT_SLICES[0])
             if next_step == (finished + 1) * STEPS_PER_CHUNK:
                 finish(finished)
                 finished += 1
+            if r == LAST:
+                quantise_basis(r, KNOT_SLICES[0])
+                pick(r, KNOT_SLICES[1])
+                multiply(LAST - 2)
+                multiply(LAST - 1)
+                multiply(LAST, [0])
+                to_basis(r, KNOT_SLICES[1])
+                quantise_basis(r, KNOT_SLICES[1])
+                multiply(LAST, [1])
+                finish(finished)
+                continue
             if is_step(r - 1):
                 to_basis(r - 1)
-            if is_step(r):
-                pick(r)
+            pick(r)
             if is_step(r - 1):
                 quantise_basis(r - 1)
-            if 0 <= r - 2 < GRID:
-                quantise_weights(r - 2)
-            if is_step(r) and pair == 1:
+            if is_step(r + 2):
+                vector_folds(r + 2)
+            if 0 <= r - 3 < GRID and r % 2 == 1:
+                for i in range(KNOTS):
+                    quantise_weights(r - 3 + i)
+            if pair == 1:
                 quantise_x(chunk)
-            if is_step(r) and pair == 0 and chunk + 1 < CHUNKS:
+            if pair == 0 and chunk + 1 < CHUNKS:
                 split_x(chunk + 1)
             for turn in range(2):
                 last_knot = next_step % STEPS_PER_CHUNK * KNOTS + KNOTS - 1
                 if (
-                    next_step <= (r - 2 if r < STEPS else r - 1)
-                    and next_step < STEPS
+                    next_step <= r - 2
                     and last_knot + 2 <= r
                     and next_step // STEPS_PER_CHUNK == finished
                 ):
                     multiply(next_step)
                     next_step += 1
             if r < GRID:
-                turn_weights(r)
-            if is_step(r) and pair == 0 and chunk + 1 < CHUNKS:
+                turn_weights(r // 2, r % 2)
+            if pair == 0 and chunk + 1 < CHUNKS:
                 turn_x(chunk + 1)
                 if chunk + 2 < CHUNKS:
                     load_x(chunk + 2)

@@ -30,6 +30,8 @@ BANKS = KNOTS * TILES
 ALL_COLS = slice(0, STEP_COLS)
 KNOT_SLICES = [slice(i * KNOT_COLS, (i + 1) * KNOT_COLS) for i in range(KNOTS)]
 LAST = STEPS - 1
+LOW, HIGH = 0, GRID - 1
+VECTOR_KNOTS = (LOW, 2, 4, HIGH)
 OUT_BLOCKS = OUTPUTS // P
 
 FLOPS = 2 * BATCH * OUTPUTS * (FEATURES * GRID + FEATURES)
@@ -69,11 +71,12 @@ def tile_advancedkanlayer_pa_kernel(
         w4_scales = keep.tile([P, OUTPUTS], U8, align_bytes=64)
         grid_rows = keep.tile([P, GRID], BF16)
         minus_grid = keep.tile([P, GRID], F32)
+        minus_one = keep.tile([P, 1], F32)
         shift = keep.tile([P, GRID], F32)
         fold_bias = keep.tile([P, GRID], F32)
 
         nc.vector.memset(w4_scales[:].bitcast(I32), 0)
-        nc.vector.memset(shift[:], -1.0)
+        nc.vector.memset(minus_one[:], -1.0)
 
         x_raw = {}
 
@@ -97,22 +100,21 @@ def tile_advancedkanlayer_pa_kernel(
                 in_=w4_scale_rows[4 * quadrant : 4 * quadrant + 4, :].bitcast(I32),
             )
 
-        LOW, HIGH = 0, GRID - 1
         nc.vector.tensor_scalar(
             out=minus_grid[:], in0=grid_rows[:], scalar1=-1.0, scalar2=None, op0=ALU.mult
         )
-        for g, sign in ((LOW, -1.0), (HIGH, 1.0)):
+        for knots, sign in ((slice(LOW, HIGH), -1.0), (slice(HIGH, GRID), 1.0)):
             nc.vector.tensor_scalar(
-                out=shift[:, g : g + 1],
-                in0=grid_rows[:, g : g + 1],
+                out=shift[:, knots],
+                in0=grid_rows[:, knots],
                 scalar1=sign,
                 scalar2=-1.0,
                 op0=ALU.mult,
                 op1=ALU.add,
             )
             nc.vector.tensor_scalar(
-                out=fold_bias[:, g : g + 1],
-                in0=grid_rows[:, g : g + 1],
+                out=fold_bias[:, knots],
+                in0=grid_rows[:, knots],
                 scalar1=-2.0 * sign,
                 scalar2=None,
                 op0=ALU.mult,
@@ -207,7 +209,15 @@ def tile_advancedkanlayer_pa_kernel(
             return 0 <= step < STEPS
 
         def on_vector(step, i):
-            return step < GRID + 2 and knots_of(step)[1][i] in (LOW, HIGH)
+            return step < GRID + 2 and knots_of(step)[1][i] in VECTOR_KNOTS
+
+        def adds_x(step, i):
+            return on_vector(step, i) or knots_of(step)[1][i] in (LOW, HIGH)
+
+        def to_gap(step, b):
+            i = b // TILES
+            g = knots_of(step)[1][i]
+            return shift[:, g : g + 1] if adds_x(step, i) else minus_one[:]
 
         def bank_cols(b):
             return slice(b * BANK, (b + 1) * BANK)
@@ -221,7 +231,7 @@ def tile_advancedkanlayer_pa_kernel(
                 nc.vector.tensor_scalar(
                     out=folded[step][:, i, :, :],
                     in0=x_split[chunk][:],
-                    scalar1=2.0 if g == LOW else -2.0,
+                    scalar1=-2.0 if g == HIGH else 2.0,
                     scalar2=fold_bias[:, g : g + 1],
                     op0=ALU.mult,
                     op1=ALU.max,
@@ -243,11 +253,11 @@ def tile_advancedkanlayer_pa_kernel(
             g = knots[i]
             bank = dist_banks.tile([P, PACK, P], F32, name="dist")
             for t in range(PACK):
-                if g in (LOW, HIGH):
+                if adds_x(step, i):
                     nc.tensor.matmul(
                         bank[:, t, :],
                         lhsT=x_split[chunk][:, j, t * P : (t + 1) * P],
-                        rhs=ident_bf16[:] if (g == LOW) != on_vector(step, i) else minus_ident[:],
+                        rhs=ident_bf16[:] if (g == HIGH) == on_vector(step, i) else minus_ident[:],
                         start=True,
                         stop=False,
                     )
@@ -255,7 +265,7 @@ def tile_advancedkanlayer_pa_kernel(
                     bank[:, t, :],
                     lhsT=folded[step][:, i, j, t * P : (t + 1) * P],
                     rhs=ident_f32[:],
-                    start=g not in (LOW, HIGH),
+                    start=not adds_x(step, i),
                     stop=True,
                     is_transpose=True,
                 )
@@ -280,24 +290,22 @@ def tile_advancedkanlayer_pa_kernel(
             )
 
         def gap_square(step, b):
-            g = knots_of(step)[1][b // TILES]
             if b == 0:
                 gap_sq[step] = f32_pool.tile([P, STEP_COLS], F32, name="gap_sq", bufs=2)
             nc.scalar.activation(
                 out=by_row(gap_sq[step][:, bank_cols(b)]),
                 in_=rows_first(dist[step, b]),
                 func=ACT.Square,
-                bias=shift[:, g : g + 1],
+                bias=to_gap(step, b),
                 scale=1.0,
             )
 
         def times_gap(step, b, out_tile, factor):
-            g = knots_of(step)[1][b // TILES]
             cols = bank_cols(b)
             nc.vector.scalar_tensor_tensor(
                 out=by_row(out_tile[:, cols]),
                 in0=rows_first(dist[step, b]),
-                scalar=shift[:, g : g + 1],
+                scalar=to_gap(step, b),
                 in1=by_row(factor[:, cols]),
                 op0=ALU.add,
                 op1=ALU.mult,
@@ -394,6 +402,10 @@ def tile_advancedkanlayer_pa_kernel(
                 if on_vector(step, i):
                     fold(step, i)
 
+        def may_multiply(step, r):
+            last_knot = step % STEPS_PER_CHUNK * KNOTS + KNOTS - 1
+            return step <= r - 2 and last_knot + 2 <= r and step // STEPS_PER_CHUNK == finished
+
         split_x(0)
         fold(0, 0)
         turn_x(0)
@@ -411,7 +423,7 @@ def tile_advancedkanlayer_pa_kernel(
         next_step = 0
         for r in range(STEPS):
             chunk, pair = divmod(r, STEPS_PER_CHUNK)
-            for product, b in ((0, 0), (1, 0), (0, 1), (1, 1), (0, 2), (0, 3), (1, 2), (1, 3)):
+            for product, b in ((0, 0), (1, 0), (0, 1), (0, 2), (1, 1), (0, 3), (1, 2), (1, 3)):
                 if product == 0:
                     inner_product(r, b)
                     inner_finish(r, b)
@@ -422,6 +434,10 @@ def tile_advancedkanlayer_pa_kernel(
                         gap_square(r + 1, b)
                     if is_step(r + 2):
                         scalar_part(r + 2, b)
+                if (product, b) == (1, 1):
+                    half_done = next_step >= STEPS_PER_CHUNK and may_multiply(next_step, r)
+                    if half_done:
+                        multiply(next_step, [0])
                 if r == LAST and (product, b) == (0, 0):
                     to_basis(r - 1)
                 if r == LAST and (product, b) == (0, 1):
@@ -436,7 +452,7 @@ def tile_advancedkanlayer_pa_kernel(
             if r == LAST:
                 quantise_basis(r, KNOT_SLICES[0])
                 pick(r, KNOT_SLICES[1])
-                multiply(LAST - 2)
+                multiply(LAST - 2, [1])
                 multiply(LAST - 1)
                 multiply(LAST, [0])
                 to_basis(r, KNOT_SLICES[1])
@@ -459,13 +475,9 @@ def tile_advancedkanlayer_pa_kernel(
             if pair == 0 and chunk + 1 < CHUNKS:
                 split_x(chunk + 1)
             for turn in range(2):
-                last_knot = next_step % STEPS_PER_CHUNK * KNOTS + KNOTS - 1
-                if (
-                    next_step <= r - 2
-                    and last_knot + 2 <= r
-                    and next_step // STEPS_PER_CHUNK == finished
-                ):
-                    multiply(next_step)
+                if may_multiply(next_step, r):
+                    multiply(next_step, [1] if half_done else [0, 1])
+                    half_done = False
                     next_step += 1
             if r < GRID:
                 turn_weights(r // 2, r % 2)

@@ -87,9 +87,10 @@ def tile_advancedkanlayer_pa_kernel(
 
         load_x(0)
         nc.sync.dma_start(out=grid_rows[:], in_=grid_points.partition_broadcast(P))
+        load_x(1)
+        load_x(2)
         for m in range(OUT_BLOCKS):
             nc.sync.dma_start(out=weight_raw[:, m, :], in_=weight_rows[:, m, :])
-        load_x(1)
         nc.sync.dma_start(
             out=w4_words[:].bitcast(I32), in_=base_activation_words.flatten_outer_dims().bitcast(I32)
         )
@@ -138,7 +139,8 @@ def tile_advancedkanlayer_pa_kernel(
                 for u in range(2):
                     nc.tensor.transpose(turned[:, j, u, :], words[:, u : FEATURES // 2 : 2], ident_f32[:])
             x_grouped[chunk] = x_pool.tile([P, KNOT_COLS], BF16, name="x_grouped", align_bytes=64)
-            nc.scalar.copy(
+            copy = nc.vector.tensor_copy if chunk <= 1 else nc.scalar.copy
+            copy(
                 out=x_grouped[chunk][:].bitcast(F32).rearrange("p (j r u) -> p j r u", j=TILES, u=2),
                 in_=turned[:].rearrange("p j u r -> p j r u"),
             )
@@ -209,7 +211,7 @@ def tile_advancedkanlayer_pa_kernel(
             return 0 <= step < STEPS
 
         def on_vector(step, i):
-            return step < GRID + 2 and knots_of(step)[1][i] in VECTOR_KNOTS
+            return step == 0 or step < GRID + 2 and knots_of(step)[1][i] in VECTOR_KNOTS
 
         def adds_x(step, i):
             return on_vector(step, i) or knots_of(step)[1][i] in (LOW, HIGH)
@@ -404,21 +406,21 @@ def tile_advancedkanlayer_pa_kernel(
 
         def may_multiply(step, r):
             last_knot = step % STEPS_PER_CHUNK * KNOTS + KNOTS - 1
-            return step <= r - 2 and last_knot + 2 <= r and step // STEPS_PER_CHUNK == finished
+            return step <= r - 2 and last_knot + 3 <= r and step // STEPS_PER_CHUNK == finished
 
         split_x(0)
         fold(0, 0)
         turn_x(0)
+        fold(0, 1)
+        vector_folds(1)
         for i in range(KNOTS):
-            if i > 0:
-                fold(0, i)
             square(0, i)
             for j in range(TILES):
                 turn_dist(0, i * TILES + j)
                 gap_square(0, i * TILES + j)
+            turn_x(1 + i)
         for n in range(BANKS):
             scalar_part(1, n)
-        vector_folds(1)
         finished = 0
         next_step = 0
         for r in range(STEPS):
@@ -467,9 +469,8 @@ def tile_advancedkanlayer_pa_kernel(
                 quantise_basis(r - 1)
             if is_step(r + 2):
                 vector_folds(r + 2)
-            if 0 <= r - 3 < GRID and r % 2 == 1:
-                for i in range(KNOTS):
-                    quantise_weights(r - 3 + i)
+            if 0 <= r - 3 < GRID:
+                quantise_weights(r - 3)
             if pair == 1:
                 quantise_x(chunk)
             if pair == 0 and chunk + 1 < CHUNKS:
@@ -481,10 +482,10 @@ def tile_advancedkanlayer_pa_kernel(
                     next_step += 1
             if r < GRID:
                 turn_weights(r // 2, r % 2)
-            if pair == 0 and chunk + 1 < CHUNKS:
+            if pair == 0 and chunk >= 2 and chunk + 1 < CHUNKS:
                 turn_x(chunk + 1)
-                if chunk + 2 < CHUNKS:
-                    load_x(chunk + 2)
+            if pair == 0 and chunk + 3 < CHUNKS:
+                load_x(chunk + 3)
             for c in range(CHUNKS):
                 if r == max(c * STEPS_PER_CHUNK + 2, GRID + 1 + c):
                     base_product(c)

from contextlib import ExitStack

import concourse.mybir as mybir
from concourse.masks import make_identity

F32 = mybir.dt.float32
BF16 = mybir.dt.bfloat16
U8 = mybir.dt.uint8
U32 = mybir.dt.uint32
I32 = mybir.dt.int32
FP8X4 = mybir.dt.float8_e4m3fn_x4
FP4X4 = mybir.dt.float4_e2m1fn_x4
ACT = mybir.ActivationFunctionType
ALU = mybir.AluOpType

P = 128
PACK = 4
BATCH, FEATURES, OUTPUTS, GRID = 2048, 512, 512, 8
ROW_TILES = BATCH // P
TILES = 2
CHUNKS = ROW_TILES // TILES
ROWS = TILES * P
KNOTS = 2
STEPS_PER_CHUNK = GRID // KNOTS
STEPS = CHUNKS * STEPS_PER_CHUNK
BANK = P * PACK
KNOT_COLS = TILES * BANK
STEP_COLS = KNOTS * KNOT_COLS
BANKS = KNOTS * TILES
ALL_COLS = slice(0, STEP_COLS)
KNOT_SLICES = [slice(i * KNOT_COLS, (i + 1) * KNOT_COLS) for i in range(KNOTS)]
LAST = STEPS - 1
LOW, HIGH = 0, GRID - 1
VECTOR_KNOTS = (LOW, 2, 4, HIGH)
OUT_BLOCKS = OUTPUTS // P

FLOPS = 2 * BATCH * OUTPUTS * (FEATURES * GRID + FEATURES)


def tile_advancedkanlayer_pa_kernel(
    tc, x_norm, spline_weight, base_activation_words, base_activation_scales, grid_points, out
):
    nc = tc.nc
    x_rows = x_norm.rearrange("(p n) i -> p n i", n=ROW_TILES)
    out_rows = out.rearrange("(p n) o -> p n o", n=ROW_TILES)
    weight_rows = spline_weight.rearrange("(m p) i g -> p m (i g)", p=P)

    with ExitStack() as pools:
        keep = pools.enter_context(tc.tile_pool(name="keep", bufs=1))
        x_pool = pools.enter_context(tc.tile_pool(name="x_pool", bufs=3))
        f32_pool = pools.enter_context(tc.tile_pool(name="f32_pool", bufs=3))
        bf16_pool = pools.enter_context(tc.tile_pool(name="bf16_pool", bufs=2))
        code_pool = pools.enter_context(tc.tile_pool(name="code_pool", bufs=3))
        out_pool = pools.enter_context(tc.tile_pool(name="out_pool", bufs=2))
        sum_banks = pools.enter_context(tc.psum_pool(name="sum_banks", bufs=TILES))
        dist_banks = pools.enter_context(tc.psum_pool(name="dist_banks", bufs=BANKS))
        work_banks = pools.enter_context(tc.psum_pool(name="work_banks", bufs=2))
        pools.enter_context(tc.manual_schedule())

        ident_f32 = keep.tile([P, P], F32)
        make_identity(nc, ident_f32[:])
        ident_bf16 = keep.tile([P, P], BF16)
        make_identity(nc, ident_bf16[:])
        minus_ident = keep.tile([P, P], BF16)
        nc.vector.tensor_scalar(out=minus_ident[:], in0=ident_bf16[:], scalar1=-1.0, scalar2=None, op0=ALU.mult)

        weight_raw = keep.tile([P, OUT_BLOCKS, FEATURES * GRID], BF16)
        weight_codes = keep.tile([P, GRID, OUTPUTS], U32, align_bytes=64)
        weight_scales = keep.tile([P, GRID, OUTPUTS], U8, align_bytes=64)
        w4_words = keep.tile([P, 2 * OUTPUTS], U8, align_bytes=64)
        w4_scales = keep.tile([P, OUTPUTS], U8, align_bytes=64)
        grid_rows = keep.tile([P, GRID], BF16)
        minus_grid = keep.tile([P, GRID], F32)
        minus_one = keep.tile([P, 1], F32)
        shift = keep.tile([P, GRID], F32)
        fold_bias = keep.tile([P, GRID], F32)

        nc.vector.memset(w4_scales[:].bitcast(I32), 0)
        nc.vector.memset(minus_one[:], -1.0)

        x_raw = {}

        def load_x(chunk):
            x_raw[chunk] = x_pool.tile([P, TILES, FEATURES], BF16, name="x_raw")
            first = chunk * TILES
            nc.sync.dma_start(out=x_raw[chunk][:], in_=x_rows[:, first : first + TILES, :])

        load_x(0)
        nc.sync.dma_start(out=grid_rows[:], in_=grid_points.partition_broadcast(P))
        load_x(1)
        load_x(2)
        for m in range(OUT_BLOCKS):
            nc.sync.dma_start(out=weight_raw[:, m, :], in_=weight_rows[:, m, :])
        nc.sync.dma_start(
            out=w4_words[:].bitcast(I32), in_=base_activation_words.flatten_outer_dims().bitcast(I32)
        )
        w4_scale_rows = base_activation_scales.flatten_outer_dims()
        for quadrant in range(4):
            nc.sync.dma_start(
                out=w4_scales[32 * quadrant : 32 * quadrant + 4, :].bitcast(I32),
                in_=w4_scale_rows[4 * quadrant : 4 * quadrant + 4, :].bitcast(I32),
            )

        nc.vector.tensor_scalar(
            out=minus_grid[:], in0=grid_rows[:], scalar1=-1.0, scalar2=None, op0=ALU.mult
        )
        for knots, sign in ((slice(LOW, HIGH), -1.0), (slice(HIGH, GRID), 1.0)):
            nc.vector.tensor_scalar(
                out=shift[:, knots],
                in0=grid_rows[:, knots],
                scalar1=sign,
                scalar2=-1.0,
                op0=ALU.mult,
                op1=ALU.add,
            )
            nc.vector.tensor_scalar(
                out=fold_bias[:, knots],
                in0=grid_rows[:, knots],
                scalar1=-2.0 * sign,
                scalar2=None,
                op0=ALU.mult,
            )

        x_grouped, x_codes, x_scales, base_sum, base_tenth = {}, {}, {}, {}, {}

        x_split = {}

        def split_x(chunk):
            x_split[chunk] = x_pool.tile([P, TILES, FEATURES], BF16, name="x_split")
            nc.vector.tensor_copy(
                out=x_split[chunk][:].rearrange("p j (t q) -> p j t q", t=PACK),
                in_=x_raw[chunk][:].rearrange("p j (q t) -> p j t q", t=PACK),
            )

        def turn_x(chunk):
            turned = work_banks.tile([P, TILES, 2, P], F32, tag="bank")
            for j in range(TILES):
                words = x_raw[chunk][:, j, :].bitcast(F32)
                for u in range(2):
                    nc.tensor.transpose(turned[:, j, u, :], words[:, u : FEATURES // 2 : 2], ident_f32[:])
            x_grouped[chunk] = x_pool.tile([P, KNOT_COLS], BF16, name="x_grouped", align_bytes=64)
            copy = nc.vector.tensor_copy if chunk <= 1 else nc.scalar.copy
            copy(
                out=x_grouped[chunk][:].bitcast(F32).rearrange("p (j r u) -> p j r u", j=TILES, u=2),
                in_=turned[:].rearrange("p j u r -> p j r u"),
            )

        def quantise_x(chunk):
            x_codes[chunk] = code_pool.tile([P, ROWS], U32, name="x_codes", align_bytes=64)
            x_scales[chunk] = code_pool.tile([P, ROWS], U8, name="x_scales", align_bytes=64)
            nc.vector.quantize_mx(
                out=x_codes[chunk][:].bitcast(FP8X4), scales=x_scales[chunk][:], in_=x_grouped[chunk][:]
            )

        def base_product(chunk):
            for j in range(TILES):
                rows = slice(j * P, (j + 1) * P)
                base_sum[chunk, j] = work_banks.tile([P, OUTPUTS], F32, name="base_sum", tag="bank")
                nc.tensor.matmul_mx(
                    out=base_sum[chunk, j][:],
                    lhsT=x_codes[chunk][:, rows].bitcast(FP8X4),
                    lhsT_scale=x_scales[chunk][:, rows],
                    rhs=w4_words[:].bitcast(FP4X4),
                    rhs_scale=w4_scales[:],
                    start=True,
                    stop=True,
                )

        def base_finish(chunk):
            base_tenth[chunk] = out_pool.tile([P, TILES, OUTPUTS], F32, name="base_tenth", bufs=3)
            for j in range(TILES):
                nc.scalar.mul(out=base_tenth[chunk][:, j, :], in_=base_sum[chunk, j][:], mul=0.1)

        weight_grouped = {}

        def turn_weights(pair, half):
            if half == 0:
                for e in range(2):
                    weight_grouped[2 * pair + e] = bf16_pool.tile(
                        [P, OUTPUTS, PACK], BF16, name="weight_grouped", align_bytes=64, bufs=4
                    )
            for m in range(2 * half, 2 * half + 2):
                words = weight_raw[:, m, :].bitcast(F32)
                turned = work_banks.tile([P, PACK, P], F32, tag="bank")
                for t in range(PACK):
                    nc.tensor.transpose(
                        turned[:, t, :], words[:, 4 * t + pair : FEATURES * GRID // 2 : 4 * PACK], ident_f32[:]
                    )
                values = turned[:].rearrange("p t o -> p (t o)").bitcast(BF16)
                values = values.rearrange("p (t o e) -> p e o t", t=PACK, e=2)
                for e in range(2):
                    nc.scalar.copy(
                        out=weight_grouped[2 * pair + e][:, m * P : (m + 1) * P, :], in_=values[:, e, :, :]
                    )

        def quantise_weights(g):
            nc.vector.quantize_mx(
                out=weight_codes[:, g, :].bitcast(FP8X4),
                scales=weight_scales[:, g, :],
                in_=weight_grouped[g][:].rearrange("p o t -> p (o t)"),
            )

        folded, dist, dist_sq, gap_sq = {}, {}, {}, {}
        inner, outer, basis, basis_codes, basis_scales = {}, {}, {}, {}, {}

        def knots_of(step):
            chunk, pair = divmod(step, STEPS_PER_CHUNK)
            return chunk, [pair * KNOTS + i for i in range(KNOTS)]

        def is_step(step):
            return 0 <= step < STEPS

        def on_vector(step, i):
            return step == 0 or step < GRID + 2 and knots_of(step)[1][i] in VECTOR_KNOTS

        def adds_x(step, i):
            return on_vector(step, i) or knots_of(step)[1][i] in (LOW, HIGH)

        def to_gap(step, b):
            i = b // TILES
            g = knots_of(step)[1][i]
            return shift[:, g : g + 1] if adds_x(step, i) else minus_one[:]

        def bank_cols(b):
            return slice(b * BANK, (b + 1) * BANK)

        def fold(step, i):
            chunk, knots = knots_of(step)
            g = knots[i]
            if step not in folded:
                folded[step] = f32_pool.tile([P, KNOTS, TILES, FEATURES], F32, name="folded", bufs=2)
            if on_vector(step, i):
                nc.vector.tensor_scalar(
                    out=folded[step][:, i, :, :],
                    in0=x_split[chunk][:],
                    scalar1=-2.0 if g == HIGH else 2.0,
                    scalar2=fold_bias[:, g : g + 1],
                    op0=ALU.mult,
                    op1=ALU.max,
                )
                return
            if g == LOW:
                func, bias, scale = ACT.Relu, fold_bias[:, g : g + 1], -2.0
            elif g == HIGH:
                func, bias, scale = ACT.Relu, fold_bias[:, g : g + 1], 2.0
            else:
                func, bias, scale = ACT.Abs, minus_grid[:, g : g + 1], 1.0
            nc.scalar.activation(
                out=folded[step][:, i, :, :], in_=x_split[chunk][:], func=func, bias=bias, scale=scale
            )

        def turn_dist(step, b):
            chunk, knots = knots_of(step)
            i, j = divmod(b, TILES)
            g = knots[i]
            bank = dist_banks.tile([P, PACK, P], F32, name="dist")
            for t in range(PACK):
                if adds_x(step, i):
                    nc.tensor.matmul(
                        bank[:, t, :],
                        lhsT=x_split[chunk][:, j, t * P : (t + 1) * P],
                        rhs=ident_bf16[:] if (g == HIGH) == on_vector(step, i) else minus_ident[:],
                        start=True,
                        stop=False,
                    )
                nc.tensor.matmul(
                    bank[:, t, :],
                    lhsT=folded[step][:, i, j, t * P : (t + 1) * P],
                    rhs=ident_f32[:],
                    start=not adds_x(step, i),
                    stop=True,
                    is_transpose=True,
                )
            dist[step, b] = bank

        def rows_first(bank):
            return bank[:].rearrange("p t r -> p r t")

        def by_row(tile_cols):
            return tile_cols.rearrange("p (r t) -> p r t", t=PACK)

        def square(step, i):
            chunk, knots = knots_of(step)
            if i == 0:
                dist_sq[step] = f32_pool.tile([P, STEP_COLS], F32, name="dist_sq")
            nc.scalar.activation(
                out=dist_sq[step][:, i * KNOT_COLS : (i + 1) * KNOT_COLS],
                in_=x_grouped[chunk][:],
                func=ACT.Square,
                bias=minus_grid[:, knots[i] : knots[i] + 1],
                scale=1.0,
            )

        def gap_square(step, b):
            if b == 0:
                gap_sq[step] = f32_pool.tile([P, STEP_COLS], F32, name="gap_sq", bufs=2)
            nc.scalar.activation(
                out=by_row(gap_sq[step][:, bank_cols(b)]),
                in_=rows_first(dist[step, b]),
                func=ACT.Square,
                bias=to_gap(step, b),
                scale=1.0,
            )

        def times_gap(step, b, out_tile, factor):
            cols = bank_cols(b)
            nc.vector.scalar_tensor_tensor(
                out=by_row(out_tile[:, cols]),
                in0=rows_first(dist[step, b]),
                scalar=to_gap(step, b),
                in1=by_row(factor[:, cols]),
                op0=ALU.add,
                op1=ALU.mult,
            )

        def inner_product(step, b):
            times_gap(step, b, dist_sq[step], dist_sq[step])

        def inner_finish(step, b):
            if b == 0:
                inner[step] = bf16_pool.tile([P, STEP_COLS], BF16, name="inner", bufs=3)
            nc.gpsimd.tensor_scalar(
                out=inner[step][:, bank_cols(b)],
                in0=dist_sq[step][:, bank_cols(b)],
                scalar1=-3.0,
                scalar2=-0.5,
                op0=ALU.mult,
                op1=ALU.add,
            )

        def outer_cubic(step, b):
            if b == 0:
                outer[step] = bf16_pool.tile([P, STEP_COLS], BF16, name="outer", bufs=3)
            times_gap(step, b, outer[step], gap_sq[step])

        def pick(step, cols=ALL_COLS):
            nc.vector.tensor_tensor(
                out=inner[step][:, cols], in0=inner[step][:, cols], in1=outer[step][:, cols], op=ALU.max
            )

        def to_basis(step, cols=ALL_COLS):
            if cols.start == 0:
                basis[step] = bf16_pool.tile([P, STEP_COLS], BF16, name="basis", align_bytes=64)
            nc.vector.tensor_scalar(
                out=basis[step][:, cols], in0=inner[step][:, cols], scalar1=0.0, scalar2=None, op0=ALU.min
            )

        def quantise_basis(step, cols=ALL_COLS):
            if cols.start == 0:
                basis_codes[step] = code_pool.tile(
                    [P, KNOTS * ROWS], U32, name="basis_codes", align_bytes=64, bufs=7
                )
                basis_scales[step] = code_pool.tile(
                    [P, KNOTS * ROWS], U8, name="basis_scales", align_bytes=64, bufs=7
                )
            words = slice(cols.start // PACK, cols.stop // PACK)
            nc.vector.quantize_mx(
                out=basis_codes[step][:, words].bitcast(FP8X4),
                scales=basis_scales[step][:, words],
                in_=basis[step][:, cols],
            )

        spline_sum = {}

        def multiply(step, which=range(KNOTS)):
            chunk, knots = knots_of(step)
            for i in which:
                g = knots[i]
                for j in range(TILES):
                    if g == 0:
                        spline_sum[j] = sum_banks.tile([P, OUTPUTS], F32, name="spline_sum")
                    rows = slice((i * TILES + j) * P, (i * TILES + j + 1) * P)
                    nc.tensor.matmul_mx(
                        out=spline_sum[j][:],
                        lhsT=basis_codes[step][:, rows].bitcast(FP8X4),
                        lhsT_scale=basis_scales[step][:, rows],
                        rhs=weight_codes[:, g, :].bitcast(FP8X4),
                        rhs_scale=weight_scales[:, g, :],
                        start=(g == 0),
                        stop=(g == GRID - 1),
                    )

        def finish(chunk):
            result = out_pool.tile([P, TILES, OUTPUTS], F32, name="result")
            for j in range(TILES):
                nc.vector.scalar_tensor_tensor(
                    out=result[:, j, :],
                    in0=spline_sum[j][:],
                    scalar=-2.0,
                    in1=base_tenth[chunk][:, j, :],
                    op0=ALU.mult,
                    op1=ALU.add,
                )
                nc.sync.dma_start(out=out_rows[:, chunk * TILES + j, :], in_=result[:, j, :])

        def scalar_part(step, n):
            if n >= KNOTS:
                square(step, n - KNOTS)
            elif not on_vector(step, n):
                fold(step, n)

        def vector_folds(step):
            for i in range(KNOTS):
                if on_vector(step, i):
                    fold(step, i)

        def may_multiply(step, r):
            last_knot = step % STEPS_PER_CHUNK * KNOTS + KNOTS - 1
            return step <= r - 2 and last_knot + 3 <= r and step // STEPS_PER_CHUNK == finished

        split_x(0)
        fold(0, 0)
        turn_x(0)
        fold(0, 1)
        vector_folds(1)
        for i in range(KNOTS):
            square(0, i)
            for j in range(TILES):
                turn_dist(0, i * TILES + j)
                gap_square(0, i * TILES + j)
            turn_x(1 + i)
        for n in range(BANKS):
            scalar_part(1, n)
        finished = 0
        next_step = 0
        for r in range(STEPS):
            chunk, pair = divmod(r, STEPS_PER_CHUNK)
            for product, b in ((0, 0), (1, 0), (0, 1), (0, 2), (1, 1), (0, 3), (1, 2), (1, 3)):
                if product == 0:
                    inner_product(r, b)
                    inner_finish(r, b)
                if product == 1:
                    outer_cubic(r, b)
                    if is_step(r + 1):
                        turn_dist(r + 1, b)
                        gap_square(r + 1, b)
                    if is_step(r + 2):
                        scalar_part(r + 2, b)
                if (product, b) == (1, 1):
                    half_done = next_step >= STEPS_PER_CHUNK and may_multiply(next_step, r)
                    if half_done:
                        multiply(next_step, [0])
                if r == LAST and (product, b) == (0, 0):
                    to_basis(r - 1)
                if r == LAST and (product, b) == (0, 1):
                    quantise_basis(r - 1)
                if r == LAST and (product, b) == (0, 3):
                    pick(r, KNOT_SLICES[0])
                if r == LAST and (product, b) == (1, 2):
                    to_basis(r, KNOT_SLICES[0])
            if next_step == (finished + 1) * STEPS_PER_CHUNK:
                finish(finished)
                finished += 1
            if r == LAST:
                quantise_basis(r, KNOT_SLICES[0])
                pick(r, KNOT_SLICES[1])
                multiply(LAST - 2, [1])
                multiply(LAST - 1)
                multiply(LAST, [0])
                to_basis(r, KNOT_SLICES[1])
                quantise_basis(r, KNOT_SLICES[1])
                multiply(LAST, [1])
                finish(finished)
                continue
            if is_step(r - 1):
                to_basis(r - 1)
            pick(r)
            if is_step(r - 1):
                quantise_basis(r - 1)
            if is_step(r + 2):
                vector_folds(r + 2)
            if 0 <= r - 3 < GRID:
                quantise_weights(r - 3)
            if pair == 1:
                quantise_x(chunk)
            if pair == 0 and chunk + 1 < CHUNKS:
                split_x(chunk + 1)
            for turn in range(2):
                if may_multiply(next_step, r):
                    multiply(next_step, [1] if half_done else [0, 1])
                    half_done = False
                    next_step += 1
            if r < GRID:
                turn_weights(r // 2, r % 2)
            if pair == 0 and chunk >= 2 and chunk + 1 < CHUNKS:
                turn_x(chunk + 1)
            if pair == 0 and chunk + 3 < CHUNKS:
                load_x(chunk + 3)
            for c in range(CHUNKS):
                if r == max(c * STEPS_PER_CHUNK + 2, GRID + 1 + c):
                    base_product(c)
                    base_finish(c)
